import numpy as np
import ml_dtypes


def mxq(x, axis, fmt="e4m3"):
    dtype, down = {"e4m3": (ml_dtypes.float8_e4m3fn, 7), "e5m2": (ml_dtypes.float8_e5m2, 14)}[fmt]
    v = np.moveaxis(np.asarray(x, np.float32).astype(ml_dtypes.bfloat16).astype(np.float64), axis, -1)
    blocks = v.reshape(v.shape[:-1] + (-1, 32))
    amax = np.abs(blocks).max(-1, keepdims=True)
    byte = np.maximum(np.where(amax > 0, np.frexp(amax)[1] - 1 + 127, 0) - down, 1)
    scale = np.exp2(byte - 127.0)
    codes = (blocks / scale).astype(np.float32).astype(dtype).astype(np.float64)
    return np.moveaxis((codes * scale).reshape(v.shape), -1, axis)


WIDE = False


def mx_kscale(k):
    if not WIDE:
        return np.ones(k)
    levels = np.array([10, -10, 5, -5, 0])
    if k % 512:
        return np.exp2(np.random.permutation(np.resize(levels, k // 32))).repeat(32)
    a = np.empty((k // 512, 16))
    for p in range(k // 512):
        a[p, :8] = np.random.permutation(np.resize(levels, 8))
        for g in range(8):
            far = levels[np.abs(levels - a[p, g]) >= 10]
            a[p, g + 8] = far[np.random.randint(len(far))]
    return np.exp2(a.ravel()).repeat(32)


BF16 = ml_dtypes.bfloat16


def bf(x):
    return np.asarray(x, np.float32).astype(BF16)


def f64(x):
    return np.asarray(x).astype(np.float64)


B, S, D, H, KVH, HD = 8, 512, 512, 4, 2, 128
E = H * HD
KV = KVH * HD
EPS = 1e-6


def layernorm(u, gamma, beta):
    mu = u.mean(-1, keepdims=True)
    var = np.square(u - mu).mean(-1, keepdims=True)
    return (u - mu) / np.sqrt(var + EPS) * gamma + beta


def apply_rope(u, cos, sin):
    half = u.shape[-1] // 2
    rotated = np.concatenate([-u[..., half:], u[..., :half]], axis=-1)
    return u * cos[None, None] + rotated * sin[None, None]


def setup_inputs():
    s = mx_kscale(D)
    return {
        "x": bf(np.random.standard_normal((B, S, D)) * s),
        "cos": bf(np.random.uniform(size=(S, HD))),
        "sin": bf(np.random.uniform(size=(S, HD))),
        "Wq": bf(np.random.standard_normal((D, E)) / np.sqrt(D) / s[:, None]),
        "Wk": bf(np.random.standard_normal((D, KV)) / np.sqrt(D) / s[:, None]),
        "Wv": bf(np.random.standard_normal((D, KV)) * 2.0 / np.sqrt(D) / s[:, None]),
        "q_gamma": bf(1.0 + 0.1 * np.random.standard_normal(HD)),
        "q_beta": bf(0.1 * np.random.standard_normal(HD)),
        "k_gamma": bf(1.0 + 0.1 * np.random.standard_normal(HD)),
        "k_beta": bf(0.1 * np.random.standard_normal(HD)),
    }


def reference(x, cos, sin, Wq, Wk, Wv, q_gamma, q_beta, k_gamma, k_beta):
    xq = mxq(f64(x), 2, "e4m3")
    q = (xq @ mxq(f64(Wq), 0, "e4m3")).reshape(B, S, H, HD).transpose(0, 2, 1, 3)
    k = (xq @ mxq(f64(Wk), 0, "e4m3")).reshape(B, S, KVH, HD).transpose(0, 2, 1, 3)
    v = (xq @ mxq(f64(Wv), 0, "e4m3")).reshape(B, S, KVH, HD).transpose(0, 2, 1, 3)
    q = layernorm(q, f64(q_gamma), f64(q_beta))
    k = layernorm(k, f64(k_gamma), f64(k_beta))
    q_rot = apply_rope(q, f64(cos), f64(sin))
    k_rot = apply_rope(k, f64(cos), f64(sin))
    return q_rot, k_rot, v

@@ -1,0 +1,283 @@
+from contextlib import ExitStack
+
+import concourse.mybir as mybir
+from concourse.masks import make_identity
+
+F32 = mybir.dt.float32
+BF16 = mybir.dt.bfloat16
+U32 = mybir.dt.uint32
+U8 = mybir.dt.uint8
+FP8X4 = mybir.dt.float8_e4m3fn_x4
+ADD = mybir.AluOpType.add
+MULT = mybir.AluOpType.mult
+ACT = mybir.ActivationFunctionType
+
+P = 128
+PACK = 4
+B, S, D = 8, 512, 512
+HD = 128
+HALF = HD // 2
+Q_HEADS, KV_HEADS = 4, 2
+NORMED = Q_HEADS + KV_HEADS
+T = S // P
+BANK = 512
+W_COLS = (Q_HEADS + 2 * KV_HEADS) * HD
+EPS = 1e-6
+
+FLOPS = 2 * B * S * D * W_COLS
+
+
+def tile_gqa_flashattn_pa_t_kernel(
+    tc, x, cos, sin, Wq, Wk, Wv, q_gamma, q_beta, k_gamma, k_beta, out_0, out_1, out_2
+):
+    nc = tc.nc
+    with ExitStack() as ctx:
+        const = ctx.enter_context(tc.tile_pool(name="const", bufs=1))
+        xprep = ctx.enter_context(tc.tile_pool(name="xprep", bufs=2))
+        stats = ctx.enter_context(tc.tile_pool(name="stats", bufs=4))
+        work = ctx.enter_context(tc.tile_pool(name="work", bufs=3))
+        outs = ctx.enter_context(tc.tile_pool(name="outs", bufs=4))
+        psum_c = ctx.enter_context(tc.psum_pool(name="psum_c", bufs=1))
+        psum_x = ctx.enter_context(tc.psum_pool(name="psum_x", bufs=2))
+        psum_u = ctx.enter_context(tc.psum_pool(name="psum_u", bufs=2))
+
+        ident = const.tile([P, P], F32)
+        make_identity(nc, ident[:])
+        ones = const.tile([P, P], BF16)
+        nc.vector.memset(ones[:], 1.0)
+        eps = const.tile([P, 1], F32)
+        nc.vector.memset(eps[:], EPS)
+        vecs = const.tile([P, 4 * HD], BF16)
+        nc.vector.memset(vecs[:], 0.0)
+
+        for n, vec in enumerate((q_gamma, k_gamma, q_beta, k_beta)):
+            nc.sync.dma_start(
+                out=vecs[0:1, n * HD : (n + 1) * HD], in_=vec.rearrange("(o j) -> o j", o=1)
+            )
+        cos_sb = const.tile([P, T, HD], BF16)
+        nc.sync.dma_start(out=cos_sb[:], in_=cos.rearrange("(p t) j -> p t j", t=T))
+        sin_sb = const.tile([P, T, HD], BF16)
+        nc.sync.dma_start(out=sin_sb[:], in_=sin.rearrange("(p t) j -> p t j", t=T))
+
+        def load_x(b):
+            x_sb = const.tile([P, T * D], BF16, name="x_sb%d" % b)
+            nc.sync.dma_start(out=x_sb[:], in_=x[b].rearrange("(p t) k -> p (t k)", t=T))
+            return x_sb
+
+        def load_w(w, name):
+            cols = w.shape[1]
+            raw = const.tile([P, PACK * cols], BF16, name=name)
+            nc.sync.dma_start(out=raw[:], in_=w.rearrange("(p v) c -> p (v c)", v=PACK))
+            return raw
+
+        x_tiles = [load_x(0)]
+        wq_raw = load_w(Wq, "wq_raw")
+        wk_raw = load_w(Wk, "wk_raw")
+        wv_raw = load_w(Wv, "wv_raw")
+        for b in range(1, B):
+            x_tiles.append(load_x(b))
+
+        def quantise_x(b):
+            x_words = x_tiles[b][:].bitcast(F32)
+            grouped = xprep.tile([P, T * P * PACK], BF16, align_bytes=64)
+            grouped_words = grouped[:].bitcast(F32)
+            for pair in range(T // 2):
+                x_t = psum_x.tile([P, BANK], F32, tag="x_t")
+                for n in range(BANK // P):
+                    first = pair * BANK + (n // 2) * 2 * P + n % 2
+                    nc.tensor.transpose(
+                        x_t[:, n * P : (n + 1) * P],
+                        x_words[:, first : first + 2 * P - 1 : 2],
+                        ident[:],
+                    )
+                nc.scalar.copy(
+                    out=grouped_words[:, pair * BANK : (pair + 1) * BANK].rearrange(
+                        "p (t r u) -> p t r u", t=2, u=2
+                    ),
+                    in_=x_t[:].rearrange("p (t u r) -> p t r u", t=2, u=2),
+                )
+            codes = xprep.tile([P, T * P], U32, align_bytes=64)
+            scales = xprep.tile([P, T * P], U8, align_bytes=64)
+            nc.vector.quantize_mx(out=codes[:].bitcast(FP8X4), scales=scales[:], in_=grouped[:])
+            return codes, scales
+
+        x_mx = quantise_x(0)
+
+        w_grouped = const.tile([P, W_COLS * PACK], BF16, align_bytes=64)
+        w_codes = const.tile([P, W_COLS], U32, align_bytes=64)
+        w_scales = const.tile([P, W_COLS], U8, align_bytes=64)
+
+        def regroup_w(copy, raw, first_col, cols):
+            copy(
+                out=w_grouped[:, first_col * PACK : (first_col + cols) * PACK].rearrange(
+                    "p (c v) -> p c v", v=PACK
+                ),
+                in_=raw[:].rearrange("p (v c) -> p c v", v=PACK),
+            )
+
+        def quantise_w(first_col, cols):
+            nc.vector.quantize_mx(
+                out=w_codes[:, first_col : first_col + cols].bitcast(FP8X4),
+                scales=w_scales[:, first_col : first_col + cols],
+                in_=w_grouped[:, first_col * PACK : (first_col + cols) * PACK],
+            )
+
+        regroup_w(nc.vector.tensor_copy, wq_raw, 0, BANK)
+        regroup_w(nc.scalar.copy, wk_raw, BANK, KV_HEADS * HD)
+        regroup_w(nc.scalar.copy, wv_raw, BANK + KV_HEADS * HD, KV_HEADS * HD)
+        quantise_w(0, BANK)
+        quantise_w(BANK, BANK)
+
+        sin_src = const.tile([P, T, HD], BF16)
+        nc.scalar.copy(out=sin_src[:, :, 0:HALF], in_=sin_sb[:, :, HALF:HD])
+        nc.scalar.mul(out=sin_src[:, :, HALF:HD], in_=sin_sb[:, :, 0:HALF], mul=-1.0)
+
+        spread = psum_x.tile([P, 4 * HD], F32, tag="x_t")
+        nc.tensor.matmul(out=spread[:], lhsT=ones[:], rhs=vecs[:], start=True, stop=True)
+
+        def scale_tables(dst, vec_pair):
+            shape = [P, T, 2, HD]
+            vec_view = vec_pair.rearrange("p (o k j) -> p o k j", o=1, k=2).to_broadcast(shape)
+            for n, table in enumerate((cos_sb, sin_src)):
+                nc.vector.tensor_tensor(
+                    out=dst[:, :, :, n, :],
+                    in0=table[:].unsqueeze(2).to_broadcast(shape),
+                    in1=vec_view,
+                    op=MULT,
+                )
+
+        def add_rotated(dst, products):
+            nc.gpsimd.tensor_tensor(
+                out=dst[:, :, 0:HALF],
+                in0=products[:, :, 0, 0:HALF],
+                in1=products[:, :, 1, HALF:HD],
+                op=ADD,
+            )
+            nc.gpsimd.tensor_tensor(
+                out=dst[:, :, HALF:HD],
+                in0=products[:, :, 0, HALF:HD],
+                in1=products[:, :, 1, 0:HALF],
+                op=ADD,
+            )
+
+        tab_ab = const.tile([P, T, 2, 2, HD], F32)
+        scale_tables(tab_ab, spread[:, 0 : 2 * HD])
+        tab_beta = const.tile([P, T, 2, 2, HD], F32)
+        scale_tables(tab_beta, spread[:, 2 * HD : 4 * HD])
+        c_sb = const.tile([P, T, 2, HD], F32)
+        add_rotated(
+            c_sb[:].rearrange("p t k j -> p (t k) j"),
+            tab_beta[:].rearrange("p t k n j -> p (t k) n j"),
+        )
+        c_ps = []
+        for pair in range(T // 2):
+            c_bank = psum_c.tile([P, 2, 2, HD], F32, name="c_bank%d" % pair)
+            nc.tensor.matmul(
+                out=c_bank[:].rearrange("p t k j -> p (t k j)"),
+                lhsT=ident[:],
+                rhs=c_sb[:, 2 * pair : 2 * pair + 2].rearrange("p t k j -> p (t k j)"),
+                start=True,
+                stop=True,
+            )
+            c_ps.append(c_bank)
+
+        def kind_of(h):
+            return 0 if h < Q_HEADS else 1
+
+        def products(b, t, x_codes, x_scales):
+            token_cols = slice(t * P, (t + 1) * P)
+            banks = []
+            for n, tag in enumerate(("u_q", "u_kv")):
+                bank = psum_u.tile([P, BANK], F32, tag=tag, name=tag)
+                nc.tensor.matmul_mx(
+                    out=bank[:],
+                    lhsT=x_codes[:, token_cols].bitcast(FP8X4),
+                    lhsT_scale=x_scales[:, token_cols],
+                    rhs=w_codes[:, n * BANK : (n + 1) * BANK].bitcast(FP8X4),
+                    rhs_scale=w_scales[:, n * BANK : (n + 1) * BANK],
+                    start=True,
+                    stop=True,
+                )
+                banks.append(bank)
+            u_kv = banks[1]
+
+            def head(h):
+                col = (h % Q_HEADS) * HD
+                return banks[kind_of(h)][:, col : col + HD]
+
+            neg_mean = stats.tile([P, NORMED], F32)
+            sum_sq = stats.tile([P, NORMED], F32)
+            unread = work.tile([P, 2 * NORMED, HD], BF16)
+            pair_ab = work.tile([P, NORMED, 2, HD], F32)
+            for heads in (range(Q_HEADS), range(Q_HEADS, NORMED)):
+                for h in heads:
+                    nc.scalar.activation(
+                        out=unread[:, h, :],
+                        in_=head(h),
+                        func=ACT.Copy,
+                        scale=-1.0 / HD,
+                        accum_out=neg_mean[:, h : h + 1],
+                    )
+                for h in heads:
+                    nc.scalar.activation(
+                        out=unread[:, NORMED + h, :],
+                        in_=head(h),
+                        func=ACT.Square,
+                        bias=neg_mean[:, h : h + 1],
+                        scale=1.0,
+                        accum_out=sum_sq[:, h : h + 1],
+                    )
+                if heads[0] == Q_HEADS:
+                    v_sb = outs.tile([P, KV_HEADS, HD], F32)
+                    nc.scalar.copy(
+                        out=v_sb[:].rearrange("p h j -> p (h j)"), in_=u_kv[:, KV_HEADS * HD : BANK]
+                    )
+                    nc.sync.dma_start(
+                        out=out_2[b].rearrange("h (p t) j -> t p h j", t=T)[t], in_=v_sb[:]
+                    )
+                for h in heads:
+                    nc.vector.scalar_tensor_tensor(
+                        out=pair_ab[:, h, :, :],
+                        in0=head(h).unsqueeze(1).to_broadcast([P, 2, HD]),
+                        scalar=neg_mean[:, h : h + 1],
+                        in1=tab_ab[:, t, kind_of(h), :, :],
+                        op0=ADD,
+                        op1=MULT,
+                    )
+            std = stats.tile([P, NORMED], F32)
+            nc.scalar.activation(
+                out=std[:], in_=sum_sq[:], func=ACT.Sqrt, bias=eps[:, 0:1], scale=1.0 / HD
+            )
+            rotated = work.tile([P, NORMED, HD], F32)
+            add_rotated(rotated, pair_ab)
+            return rotated, std
+
+        def finish(b, t, rotated, std):
+            rstd = stats.tile([P, NORMED], F32)
+            nc.vector.reciprocal(out=rstd[:], in_=std[:])
+            q_sb = outs.tile([P, Q_HEADS, HD], F32)
+            k_sb = outs.tile([P, KV_HEADS, HD], F32)
+            for h in range(NORMED):
+                dst = q_sb[:, h, :] if h < Q_HEADS else k_sb[:, h - Q_HEADS, :]
+                nc.vector.scalar_tensor_tensor(
+                    out=dst,
+                    in0=rotated[:, h, :],
+                    scalar=rstd[:, h : h + 1],
+                    in1=c_ps[t // 2][:, t % 2, kind_of(h), :],
+                    op0=MULT,
+                    op1=ADD,
+                )
+            nc.sync.dma_start(out=out_0[b].rearrange("h (p t) j -> t p h j", t=T)[t], in_=q_sb[:])
+            nc.sync.dma_start(out=out_1[b].rearrange("h (p t) j -> t p h j", t=T)[t], in_=k_sb[:])
+
+        waiting = None
+        for b in range(B):
+            x_codes, x_scales = x_mx
+            for t in range(T):
+                made = products(b, t, x_codes, x_scales)
+                if t == 0 and b + 1 < B:
+                    x_mx = quantise_x(b + 1)
+                if waiting is not None:
+                    finish(*waiting)
+                waiting = (b, t) + made
+        finish(*waiting)

@@ -7,6 +7,7 @@ F32 = mybir.dt.float32
 BF16 = mybir.dt.bfloat16
 U32 = mybir.dt.uint32
 U8 = mybir.dt.uint8
+I32 = mybir.dt.int32
 FP8X4 = mybir.dt.float8_e4m3fn_x4
 ADD = mybir.AluOpType.add
 MULT = mybir.AluOpType.mult
@@ -14,6 +15,7 @@ ACT = mybir.ActivationFunctionType
 
 P = 128
 PACK = 4
+RUN = 16
 B, S, D = 8, 512, 512
 HD = 128
 HALF = HD // 2
@@ -23,6 +25,11 @@ T = S // P
 BANK = 512
 W_COLS = (Q_HEADS + 2 * KV_HEADS) * HD
 EPS = 1e-6
+HEADS = Q_HEADS + 2 * KV_HEADS
+RUNS = HD // RUN
+GP_HEADS = range(Q_HEADS, NORMED)
+TILES = B * T
+LAG = 3
 
 FLOPS = 2 * B * S * D * W_COLS
 
@@ -33,79 +40,67 @@ def tile_gqa_flashattn_pa_t_kernel(
     nc = tc.nc
     with ExitStack() as ctx:
         const = ctx.enter_context(tc.tile_pool(name="const", bufs=1))
-        xprep = ctx.enter_context(tc.tile_pool(name="xprep", bufs=2))
-        stats = ctx.enter_context(tc.tile_pool(name="stats", bufs=4))
+        xprep = ctx.enter_context(tc.tile_pool(name="xprep", bufs=4))
+        stats = ctx.enter_context(tc.tile_pool(name="stats", bufs=8))
         work = ctx.enter_context(tc.tile_pool(name="work", bufs=3))
         outs = ctx.enter_context(tc.tile_pool(name="outs", bufs=4))
         psum_c = ctx.enter_context(tc.psum_pool(name="psum_c", bufs=1))
-        psum_x = ctx.enter_context(tc.psum_pool(name="psum_x", bufs=2))
+        psum_x = ctx.enter_context(tc.psum_pool(name="psum_x", bufs=1))
+        psum_m = ctx.enter_context(tc.psum_pool(name="psum_m", bufs=1))
         psum_u = ctx.enter_context(tc.psum_pool(name="psum_u", bufs=2))
+        ctx.enter_context(tc.manual_schedule())
 
-        ident = const.tile([P, P], F32)
-        make_identity(nc, ident[:])
-        ones = const.tile([P, P], BF16)
-        nc.vector.memset(ones[:], 1.0)
-        eps = const.tile([P, 1], F32)
-        nc.vector.memset(eps[:], EPS)
         vecs = const.tile([P, 4 * HD], BF16)
         nc.vector.memset(vecs[:], 0.0)
+        eps = const.tile([P, 1], F32)
+        nc.vector.memset(eps[:], EPS)
+        ones = const.tile([P, P], BF16)
+        nc.vector.memset(ones[:], 1.0)
+        ident = const.tile([P, P], F32)
+        make_identity(nc, ident[:])
+        warm = const.tile([P, 1], F32)
+        nc.scalar.activation(out=warm[:], in_=eps[:], func=ACT.Abs_reciprocal_sqrt)
 
         for n, vec in enumerate((q_gamma, k_gamma, q_beta, k_beta)):
-            nc.sync.dma_start(
+            nc.scalar.dma_start(
                 out=vecs[0:1, n * HD : (n + 1) * HD], in_=vec.rearrange("(o j) -> o j", o=1)
             )
+
+        def load_w(w, name):
+            raw = const.tile([P, PACK * w.shape[1]], BF16, name=name)
+            nc.sync.dma_start(out=raw[:], in_=w.rearrange("(p v) c -> p (v c)", v=PACK))
+            return raw
+
+        def load_x(b, pair):
+            x_sb = const.tile([P, 2 * D], BF16, name="x_sb%d_%d" % (b, pair))
+            nc.sync.dma_start(
+                out=x_sb[:], in_=x[b].rearrange("(p h t) k -> h p (t k)", h=2, t=2)[pair]
+            )
+            return x_sb
+
+        wq_raw = load_w(Wq, "wq_raw")
         cos_sb = const.tile([P, T, HD], BF16)
         nc.sync.dma_start(out=cos_sb[:], in_=cos.rearrange("(p t) j -> p t j", t=T))
         sin_sb = const.tile([P, T, HD], BF16)
         nc.sync.dma_start(out=sin_sb[:], in_=sin.rearrange("(p t) j -> p t j", t=T))
-
-        def load_x(b):
-            x_sb = const.tile([P, T * D], BF16, name="x_sb%d" % b)
-            nc.sync.dma_start(out=x_sb[:], in_=x[b].rearrange("(p t) k -> p (t k)", t=T))
-            return x_sb
-
-        def load_w(w, name):
-            cols = w.shape[1]
-            raw = const.tile([P, PACK * cols], BF16, name=name)
-            nc.sync.dma_start(out=raw[:], in_=w.rearrange("(p v) c -> p (v c)", v=PACK))
-            return raw
-
-        x_tiles = [load_x(0)]
-        wq_raw = load_w(Wq, "wq_raw")
         wk_raw = load_w(Wk, "wk_raw")
         wv_raw = load_w(Wv, "wv_raw")
-        for b in range(1, B):
-            x_tiles.append(load_x(b))
+        x_tiles = [[load_x(b, pair) for pair in range(2)] for b in range(B)]
 
-        def quantise_x(b):
-            x_words = x_tiles[b][:].bitcast(F32)
-            grouped = xprep.tile([P, T * P * PACK], BF16, align_bytes=64)
-            grouped_words = grouped[:].bitcast(F32)
-            for pair in range(T // 2):
-                x_t = psum_x.tile([P, BANK], F32, tag="x_t")
-                for n in range(BANK // P):
-                    first = pair * BANK + (n // 2) * 2 * P + n % 2
-                    nc.tensor.transpose(
-                        x_t[:, n * P : (n + 1) * P],
-                        x_words[:, first : first + 2 * P - 1 : 2],
-                        ident[:],
-                    )
-                nc.scalar.copy(
-                    out=grouped_words[:, pair * BANK : (pair + 1) * BANK].rearrange(
-                        "p (t r u) -> p t r u", t=2, u=2
-                    ),
-                    in_=x_t[:].rearrange("p (t u r) -> p t r u", t=2, u=2),
-                )
-            codes = xprep.tile([P, T * P], U32, align_bytes=64)
-            scales = xprep.tile([P, T * P], U8, align_bytes=64)
-            nc.vector.quantize_mx(out=codes[:].bitcast(FP8X4), scales=scales[:], in_=grouped[:])
-            return codes, scales
-
-        x_mx = quantise_x(0)
+        signs = const.tile([P, 3, P], BF16)
+        nc.vector.tensor_copy(out=signs[:, 0, :], in_=ident[:])
+        nc.vector.tensor_copy(out=signs[:, 1, 0:HALF], in_=ident[:, HALF:HD])
+        nc.vector.tensor_copy(out=signs[:, 2, HALF:HD], in_=ident[:, HALF:HD])
+        nc.vector.tensor_scalar_mul(out=signs[:, 1, HALF:HD], in0=ident[:, 0:HALF], scalar1=-1.0)
+        nc.vector.tensor_scalar_mul(out=signs[:, 2, 0:HALF], in0=ident[:, 0:HALF], scalar1=-1.0)
+        ident_b = signs[:, 0, :]
 
         w_grouped = const.tile([P, W_COLS * PACK], BF16, align_bytes=64)
         w_codes = const.tile([P, W_COLS], U32, align_bytes=64)
         w_scales = const.tile([P, W_COLS], U8, align_bytes=64)
+        nc.gpsimd.memset(w_scales[:].bitcast(I32), 0)
+        m_codes = const.tile([P, W_COLS], U32, align_bytes=64)
+        m_scales = const.tile([P, W_COLS], U8, align_bytes=64)
 
         def regroup_w(copy, raw, first_col, cols):
             copy(
@@ -122,146 +117,236 @@ def tile_gqa_flashattn_pa_t_kernel(
                 in_=w_grouped[:, first_col * PACK : (first_col + cols) * PACK],
             )
 
-        regroup_w(nc.vector.tensor_copy, wq_raw, 0, BANK)
-        regroup_w(nc.scalar.copy, wk_raw, BANK, KV_HEADS * HD)
-        regroup_w(nc.scalar.copy, wv_raw, BANK + KV_HEADS * HD, KV_HEADS * HD)
-        quantise_w(0, BANK)
-        quantise_w(BANK, BANK)
+        def transpose_x(b, pair):
+            x_words = x_tiles[b][pair][:].bitcast(F32)
+            x_t = psum_x.tile([P, BANK], F32, tag="x_t")
+            for n in range(BANK // P):
+                first = (n // 2) * 2 * P + n % 2
+                nc.tensor.transpose(
+                    x_t[:, n * P : (n + 1) * P],
+                    x_words[:, first : first + 2 * P - 1 : 2],
+                    ident[:],
+                )
+            grouped = xprep.tile([P, 2 * P * PACK], BF16, align_bytes=64)
+            nc.scalar.copy(
+                out=grouped[:].bitcast(F32).rearrange("p (t r u) -> p t r u", t=2, u=2),
+                in_=x_t[:].rearrange("p (t u r) -> p t r u", t=2, u=2),
+            )
+            return grouped
 
-        sin_src = const.tile([P, T, HD], BF16)
-        nc.scalar.copy(out=sin_src[:, :, 0:HALF], in_=sin_sb[:, :, HALF:HD])
-        nc.scalar.mul(out=sin_src[:, :, HALF:HD], in_=sin_sb[:, :, 0:HALF], mul=-1.0)
+        def quantise_x(grouped):
+            codes = xprep.tile([P, 2 * P], U32, align_bytes=64)
+            scales = xprep.tile([P, 2 * P], U8, align_bytes=64)
+            nc.vector.quantize_mx(out=codes[:].bitcast(FP8X4), scales=scales[:], in_=grouped[:])
+            return codes, scales
 
-        spread = psum_x.tile([P, 4 * HD], F32, tag="x_t")
-        nc.tensor.matmul(out=spread[:], lhsT=ones[:], rhs=vecs[:], start=True, stop=True)
+        def sum_heads(codes, scales):
+            sums = psum_m.tile([P, 2, HEADS, RUN], F32, tag="mean")
+            for t in range(2):
+                token_cols = slice(t * P, (t + 1) * P)
+                for i in range(RUNS):
+                    cols = slice(i * P, (i + 1) * P)
+                    nc.tensor.matmul_mx(
+                        out=sums[:, t].rearrange("p h c -> p (h c)"),
+                        lhsT=codes[:, token_cols].bitcast(FP8X4),
+                        lhsT_scale=scales[:, token_cols],
+                        rhs=m_codes[:, cols].bitcast(FP8X4),
+                        rhs_scale=m_scales[:, cols],
+                        start=i == 0,
+                        stop=i == RUNS - 1,
+                    )
+            return sums
 
-        def scale_tables(dst, vec_pair):
-            shape = [P, T, 2, HD]
-            vec_view = vec_pair.rearrange("p (o k j) -> p o k j", o=1, k=2).to_broadcast(shape)
-            for n, table in enumerate((cos_sb, sin_src)):
+        def reduce_sums(sums):
+            total = stats.tile([P, 2, NORMED], F32)
+            nc.vector.tensor_reduce(
+                out=total[:], in_=sums[:, :, 0:NORMED, :], axis=mybir.AxisListType.X, op=ADD
+            )
+            return total
+
+        def negate_means(total):
+            neg_mean = stats.tile([P, 2, NORMED], F32)
+            nc.scalar.mul(out=neg_mean[:], in_=total[:], mul=-1.0 / HD)
+            return neg_mean
+
+        diag = const.tile([P, 4, 2, HD], BF16)
+        trig = const.tile([P, 2, T, P], BF16)
+        tab_ab = const.tile([P, T, 2, 2, HD], F32)
+
+        def multiply_ab(t, pool, tag):
+            ab = pool.tile([P, 2, 2 * HD], F32, tag=tag, name="ab")
+            for n in range(2):
+                nc.tensor.matmul(
+                    out=ab[:, n, :],
+                    lhsT=trig[:, n, t, :],
+                    rhs=diag[:, n].rearrange("p k j -> p (k j)"),
+                    start=True,
+                    stop=True,
+                )
+            return ab
+
+        def copy_ab(t, ab):
+            nc.scalar.copy(
+                out=tab_ab[:, t].rearrange("p n k j -> p (n k j)"),
+                in_=ab[:].rearrange("p n c -> p (n c)"),
+            )
+
+        def diagonals_for_c(spread):
+            nc.vector.tensor_tensor(
+                out=diag[:, 2],
+                in0=signs[:, 0:1, :].to_broadcast([P, 2, HD]),
+                in1=spread[:, 2:4, :],
+                op=MULT,
+            )
+            for to, other in ((slice(0, HALF), slice(HALF, HD)), (slice(HALF, HD), slice(0, HALF))):
                 nc.vector.tensor_tensor(
-                    out=dst[:, :, :, n, :],
-                    in0=table[:].unsqueeze(2).to_broadcast(shape),
-                    in1=vec_view,
+                    out=diag[:, 3, :, to],
+                    in0=signs[:, 2:3, to].to_broadcast([P, 2, HALF]),
+                    in1=spread[:, 2:4, other],
                     op=MULT,
                 )
 
-        def add_rotated(dst, products):
-            nc.gpsimd.tensor_tensor(
-                out=dst[:, :, 0:HALF],
-                in0=products[:, :, 0, 0:HALF],
-                in1=products[:, :, 1, HALF:HD],
-                op=ADD,
-            )
-            nc.gpsimd.tensor_tensor(
-                out=dst[:, :, HALF:HD],
-                in0=products[:, :, 0, HALF:HD],
-                in1=products[:, :, 1, 0:HALF],
-                op=ADD,
-            )
+        def multiply_c(pair):
+            c_bank = psum_c.tile([P, 2, 2, HD], F32, tag="c%d" % pair, name="c_bank")
+            for half in range(2):
+                for n in range(2):
+                    nc.tensor.matmul(
+                        out=c_bank[:, half].rearrange("p k j -> p (k j)"),
+                        lhsT=trig[:, n, 2 * pair + half, :],
+                        rhs=diag[:, 2 + n].rearrange("p k j -> p (k j)"),
+                        start=n == 0,
+                        stop=n == 1,
+                    )
+            return c_bank
 
-        tab_ab = const.tile([P, T, 2, 2, HD], F32)
-        scale_tables(tab_ab, spread[:, 0 : 2 * HD])
-        tab_beta = const.tile([P, T, 2, 2, HD], F32)
-        scale_tables(tab_beta, spread[:, 2 * HD : 4 * HD])
-        c_sb = const.tile([P, T, 2, HD], F32)
-        add_rotated(
-            c_sb[:].rearrange("p t k j -> p (t k) j"),
-            tab_beta[:].rearrange("p t k n j -> p (t k) n j"),
+        spread = psum_u.tile([P, 4, HD], F32, tag="u_kv")
+        nc.tensor.matmul(
+            out=spread[:].rearrange("p n j -> p (n j)"), lhsT=ones[:], rhs=vecs[:], start=True, stop=True
         )
-        c_ps = []
-        for pair in range(T // 2):
-            c_bank = psum_c.tile([P, 2, 2, HD], F32, name="c_bank%d" % pair)
-            nc.tensor.matmul(
-                out=c_bank[:].rearrange("p t k j -> p (t k j)"),
-                lhsT=ident[:],
-                rhs=c_sb[:, 2 * pair : 2 * pair + 2].rearrange("p t k j -> p (t k j)"),
-                start=True,
-                stop=True,
+        trig_t = psum_u.tile([P, 2, T, P], BF16, tag="u_q")
+        for n, table in enumerate((cos_sb, sin_sb)):
+            for t in range(T):
+                nc.tensor.transpose(trig_t[:, n, t, :], table[:, t, :], ident_b)
+        regroup_w(nc.vector.tensor_copy, wq_raw, 0, BANK)
+        nc.scalar.copy(out=trig[:], in_=trig_t[:])
+        nc.vector.tensor_tensor(
+            out=diag[:, 0:2],
+            in0=signs[:, 0:2, :].unsqueeze(2).to_broadcast([P, 2, 2, HD]),
+            in1=spread[:, 0:2, :].unsqueeze(1).to_broadcast([P, 2, 2, HD]),
+            op=MULT,
+        )
+        regroup_w(nc.scalar.copy, wk_raw, BANK, KV_HEADS * HD)
+        quantise_w(0, BANK)
+        regroup_w(nc.vector.tensor_copy, wv_raw, BANK + KV_HEADS * HD, KV_HEADS * HD)
+        x_grouped = [transpose_x(0, 0)]
+        copy_ab(0, multiply_ab(0, psum_u, "u_q"))
+        quantise_w(BANK, BANK)
+        for dst, src, per_run in ((m_codes, w_codes, RUN), (m_scales, w_scales, RUN // PACK)):
+            nc.vector.tensor_copy(
+                out=dst[:].bitcast(I32).rearrange("p (i h c) -> p h i c", h=HEADS, c=per_run),
+                in_=src[:].bitcast(I32).rearrange("p (h i c) -> p h i c", h=HEADS, c=per_run),
             )
-            c_ps.append(c_bank)
+        x_grouped.append(transpose_x(0, 1))
+        x_mx = [quantise_x(grouped) for grouped in x_grouped]
+        neg_means = [negate_means(reduce_sums(sum_heads(*x_mx[0])))]
+        ab_waiting = {1: multiply_ab(1, psum_c, "c1"), 2: multiply_ab(2, psum_c, "c0")}
 
         def kind_of(h):
             return 0 if h < Q_HEADS else 1
 
-        def products(b, t, x_codes, x_scales):
-            token_cols = slice(t * P, (t + 1) * P)
+        def project(t, codes, scales):
+            token_cols = slice(t % 2 * P, (t % 2 + 1) * P)
             banks = []
             for n, tag in enumerate(("u_q", "u_kv")):
                 bank = psum_u.tile([P, BANK], F32, tag=tag, name=tag)
                 nc.tensor.matmul_mx(
                     out=bank[:],
-                    lhsT=x_codes[:, token_cols].bitcast(FP8X4),
-                    lhsT_scale=x_scales[:, token_cols],
+                    lhsT=codes[:, token_cols].bitcast(FP8X4),
+                    lhsT_scale=scales[:, token_cols],
                     rhs=w_codes[:, n * BANK : (n + 1) * BANK].bitcast(FP8X4),
                     rhs_scale=w_scales[:, n * BANK : (n + 1) * BANK],
                     start=True,
                     stop=True,
                 )
                 banks.append(bank)
-            u_kv = banks[1]
+            return banks
 
-            def head(h):
-                col = (h % Q_HEADS) * HD
-                return banks[kind_of(h)][:, col : col + HD]
+        def head_of(banks, h):
+            col = (h % Q_HEADS) * HD
+            return banks[kind_of(h)][:, col : col + HD]
 
-            neg_mean = stats.tile([P, NORMED], F32)
+        def measure(b, t, banks, neg_mean, centred):
             sum_sq = stats.tile([P, NORMED], F32)
-            unread = work.tile([P, 2 * NORMED, HD], BF16)
-            pair_ab = work.tile([P, NORMED, 2, HD], F32)
-            for heads in (range(Q_HEADS), range(Q_HEADS, NORMED)):
-                for h in heads:
-                    nc.scalar.activation(
-                        out=unread[:, h, :],
-                        in_=head(h),
-                        func=ACT.Copy,
-                        scale=-1.0 / HD,
-                        accum_out=neg_mean[:, h : h + 1],
-                    )
-                for h in heads:
-                    nc.scalar.activation(
-                        out=unread[:, NORMED + h, :],
-                        in_=head(h),
-                        func=ACT.Square,
-                        bias=neg_mean[:, h : h + 1],
-                        scale=1.0,
-                        accum_out=sum_sq[:, h : h + 1],
-                    )
-                if heads[0] == Q_HEADS:
-                    v_sb = outs.tile([P, KV_HEADS, HD], F32)
-                    nc.scalar.copy(
-                        out=v_sb[:].rearrange("p h j -> p (h j)"), in_=u_kv[:, KV_HEADS * HD : BANK]
-                    )
-                    nc.sync.dma_start(
-                        out=out_2[b].rearrange("h (p t) j -> t p h j", t=T)[t], in_=v_sb[:]
-                    )
-                for h in heads:
-                    nc.vector.scalar_tensor_tensor(
-                        out=pair_ab[:, h, :, :],
-                        in0=head(h).unsqueeze(1).to_broadcast([P, 2, HD]),
-                        scalar=neg_mean[:, h : h + 1],
-                        in1=tab_ab[:, t, kind_of(h), :, :],
-                        op0=ADD,
-                        op1=MULT,
-                    )
-            std = stats.tile([P, NORMED], F32)
-            nc.scalar.activation(
-                out=std[:], in_=sum_sq[:], func=ACT.Sqrt, bias=eps[:, 0:1], scale=1.0 / HD
+            unread = work.tile([P, NORMED, HD], BF16)
+            for h in range(NORMED):
+                nc.scalar.activation(
+                    out=unread[:, h, :],
+                    in_=head_of(banks, h),
+                    func=ACT.Square,
+                    bias=neg_mean[:, t % 2, h : h + 1],
+                    scale=1.0,
+                    accum_out=sum_sq[:, h : h + 1],
+                )
+            for h in GP_HEADS:
+                nc.scalar.activation(
+                    out=centred[:, t % 2, h - GP_HEADS[0], :],
+                    in_=head_of(banks, h),
+                    func=ACT.Identity,
+                    bias=neg_mean[:, t % 2, h : h + 1],
+                    scale=1.0,
+                )
+            v_sb = outs.tile([P, KV_HEADS, HD], F32)
+            nc.scalar.copy(
+                out=v_sb[:].rearrange("p h j -> p (h j)"), in_=banks[1][:, KV_HEADS * HD : BANK]
             )
-            rotated = work.tile([P, NORMED, HD], F32)
-            add_rotated(rotated, pair_ab)
-            return rotated, std
-
-        def finish(b, t, rotated, std):
+            nc.sync.dma_start(out=out_2[b].rearrange("h (p t) j -> t p h j", t=T)[t], in_=v_sb[:])
             rstd = stats.tile([P, NORMED], F32)
-            nc.vector.reciprocal(out=rstd[:], in_=std[:])
+            nc.scalar.activation(
+                out=rstd[:],
+                in_=sum_sq[:],
+                func=ACT.Abs_reciprocal_sqrt,
+                bias=eps[:, 0:1],
+                scale=1.0 / HD,
+            )
+            return rstd
+
+        def products(t, banks, neg_mean, pair_ab):
+            for h in range(NORMED):
+                tables = 1 if h in GP_HEADS else 2
+                nc.vector.scalar_tensor_tensor(
+                    out=pair_ab[:, t % 2, h, 0:tables, :],
+                    in0=head_of(banks, h).unsqueeze(1).to_broadcast([P, tables, HD]),
+                    scalar=neg_mean[:, t % 2, h : h + 1],
+                    in1=tab_ab[:, t, 0:tables, kind_of(h), :],
+                    op0=ADD,
+                    op1=MULT,
+                )
+
+        def rotate(t0, count, pair_ab, centred, rotated):
+            first = t0 % 2
+            mine = slice(first, first + count)
+            heads = len(GP_HEADS)
+            nc.gpsimd.tensor_tensor(
+                out=pair_ab[:, mine, GP_HEADS[0] :, 1, :],
+                in0=centred[:, mine],
+                in1=tab_ab[:, t0 : t0 + count, 1, 1:2, :].to_broadcast([P, count, heads, HD]),
+                op=MULT,
+            )
+            pair = pair_ab[:, mine].rearrange("p t h n j -> p (t h) n j")
+            out = rotated[:, mine].rearrange("p t h j -> p (t h) j")
+            for to, other in ((slice(0, HALF), slice(HALF, HD)), (slice(HALF, HD), slice(0, HALF))):
+                nc.gpsimd.tensor_tensor(
+                    out=out[:, :, to], in0=pair[:, :, 0, to], in1=pair[:, :, 1, other], op=ADD
+                )
+
+        def finish(b, t, rotated, rstd):
             q_sb = outs.tile([P, Q_HEADS, HD], F32)
             k_sb = outs.tile([P, KV_HEADS, HD], F32)
             for h in range(NORMED):
                 dst = q_sb[:, h, :] if h < Q_HEADS else k_sb[:, h - Q_HEADS, :]
                 nc.vector.scalar_tensor_tensor(
                     out=dst,
-                    in0=rotated[:, h, :],
+                    in0=rotated[:, t % 2, h, :],
                     scalar=rstd[:, h : h + 1],
                     in1=c_ps[t // 2][:, t % 2, kind_of(h), :],
                     op0=MULT,
@@ -270,14 +355,50 @@ def tile_gqa_flashattn_pa_t_kernel(
             nc.sync.dma_start(out=out_0[b].rearrange("h (p t) j -> t p h j", t=T)[t], in_=q_sb[:])
             nc.sync.dma_start(out=out_1[b].rearrange("h (p t) j -> t p h j", t=T)[t], in_=k_sb[:])
 
-        waiting = None
-        for b in range(B):
-            x_codes, x_scales = x_mx
-            for t in range(T):
-                made = products(b, t, x_codes, x_scales)
-                if t == 0 and b + 1 < B:
-                    x_mx = quantise_x(b + 1)
-                if waiting is not None:
-                    finish(*waiting)
-                waiting = (b, t) + made
-        finish(*waiting)
+        c_ps = []
+        waiting = []
+        grouped = {}
+        sums = {}
+        totals = {}
+        x_of = {(0, 0): x_mx[0], (0, 1): x_mx[1]}
+        mean_of = {(0, 0): neg_means[0]}
+        for i in range(TILES):
+            b, t = divmod(i, T)
+            if t % 2 == 0:
+                pair_ab = work.tile([P, 2, NORMED, 2, HD], F32)
+                centred = work.tile([P, 2, len(GP_HEADS), HD], F32)
+                rotated = work.tile([P, 2, NORMED, HD], F32)
+            banks = project(t, *x_of[b, t // 2])
+            if i == 0:
+                sums[0, 1] = sum_heads(*x_of[0, 1])
+            if i == 1:
+                ab_waiting[3] = multiply_ab(3, psum_c, "c1")
+            if i in (2, 3):
+                c_ps.append(multiply_c(i - 2))
+            if b + 1 < B and t >= 2:
+                sums[b + 1, t - 2] = sum_heads(*x_of[b + 1, t - 2])
+            rstd = measure(b, t, banks, mean_of[b, t // 2], centred)
+            if i + 1 in ab_waiting:
+                copy_ab(i + 1, ab_waiting[i + 1])
+            if b + 1 < B and t < 2:
+                grouped[b + 1, t] = transpose_x(b + 1, t)
+            products(t, banks, mean_of[b, t // 2], pair_ab)
+            if i == 0:
+                diagonals_for_c(spread)
+                totals[0, 1] = reduce_sums(sums[0, 1])
+            waiting.append((b, t, rotated, rstd))
+            if t % 2 == 1:
+                rotate(t - 1, 2, pair_ab, centred, rotated)
+            if len(waiting) > LAG:
+                finish(*waiting[0])
+                waiting = waiting[1:]
+            if b + 1 < B and t < 2:
+                x_of[b + 1, t] = quantise_x(grouped[b + 1, t])
+            if b + 1 < B and t >= 2:
+                totals[b + 1, t - 2] = reduce_sums(sums[b + 1, t - 2])
+            if b + 1 < B and t == 3:
+                mean_of[b + 1, 0] = negate_means(totals[b + 1, 0])
+            if t == (0 if b > 0 else 1):
+                mean_of[b, 1] = negate_means(totals[b, 1])
+        for tile in waiting:
+            finish(*tile)

@@ -30,6 +30,7 @@ RUNS = HD // RUN
 GP_HEADS = range(Q_HEADS, NORMED)
 TILES = B * T
 LAG = 3
+LEAD = 3
 
 FLOPS = 2 * B * S * D * W_COLS
 
@@ -58,13 +59,13 @@ def tile_gqa_flashattn_pa_t_kernel(
         nc.vector.memset(ones[:], 1.0)
         ident = const.tile([P, P], F32)
         make_identity(nc, ident[:])
-        warm = const.tile([P, 1], F32)
-        nc.scalar.activation(out=warm[:], in_=eps[:], func=ACT.Abs_reciprocal_sqrt)
-
         for n, vec in enumerate((q_gamma, k_gamma, q_beta, k_beta)):
             nc.scalar.dma_start(
                 out=vecs[0:1, n * HD : (n + 1) * HD], in_=vec.rearrange("(o j) -> o j", o=1)
             )
+
+        warm = const.tile([P, 1], F32)
+        nc.scalar.activation(out=warm[:], in_=eps[:], func=ACT.Abs_reciprocal_sqrt)
 
         def load_w(w, name):
             raw = const.tile([P, PACK * w.shape[1]], BF16, name=name)
@@ -140,32 +141,31 @@ def tile_gqa_flashattn_pa_t_kernel(
             nc.vector.quantize_mx(out=codes[:].bitcast(FP8X4), scales=scales[:], in_=grouped[:])
             return codes, scales
 
-        def sum_heads(codes, scales):
-            sums = psum_m.tile([P, 2, HEADS, RUN], F32, tag="mean")
-            for t in range(2):
-                token_cols = slice(t * P, (t + 1) * P)
-                for i in range(RUNS):
-                    cols = slice(i * P, (i + 1) * P)
-                    nc.tensor.matmul_mx(
-                        out=sums[:, t].rearrange("p h c -> p (h c)"),
-                        lhsT=codes[:, token_cols].bitcast(FP8X4),
-                        lhsT_scale=scales[:, token_cols],
-                        rhs=m_codes[:, cols].bitcast(FP8X4),
-                        rhs_scale=m_scales[:, cols],
-                        start=i == 0,
-                        stop=i == RUNS - 1,
-                    )
+        def sum_heads(t, codes, scales):
+            sums = psum_m.tile([P, HEADS, RUN], F32, tag="mean")
+            token_cols = slice(t % 2 * P, (t % 2 + 1) * P)
+            for i in range(RUNS):
+                cols = slice(i * P, (i + 1) * P)
+                nc.tensor.matmul_mx(
+                    out=sums[:].rearrange("p h c -> p (h c)"),
+                    lhsT=codes[:, token_cols].bitcast(FP8X4),
+                    lhsT_scale=scales[:, token_cols],
+                    rhs=m_codes[:, cols].bitcast(FP8X4),
+                    rhs_scale=m_scales[:, cols],
+                    start=i == 0,
+                    stop=i == RUNS - 1,
+                )
             return sums
 
         def reduce_sums(sums):
-            total = stats.tile([P, 2, NORMED], F32)
+            total = stats.tile([P, NORMED], F32)
             nc.vector.tensor_reduce(
-                out=total[:], in_=sums[:, :, 0:NORMED, :], axis=mybir.AxisListType.X, op=ADD
+                out=total[:], in_=sums[:, 0:NORMED, :], axis=mybir.AxisListType.X, op=ADD
             )
             return total
 
         def negate_means(total):
-            neg_mean = stats.tile([P, 2, NORMED], F32)
+            neg_mean = stats.tile([P, NORMED], F32)
             nc.scalar.mul(out=neg_mean[:], in_=total[:], mul=-1.0 / HD)
             return neg_mean
 
@@ -247,8 +247,9 @@ def tile_gqa_flashattn_pa_t_kernel(
                 in_=src[:].bitcast(I32).rearrange("p (h i c) -> p h i c", h=HEADS, c=per_run),
             )
         x_grouped.append(transpose_x(0, 1))
-        x_mx = [quantise_x(grouped) for grouped in x_grouped]
-        neg_means = [negate_means(reduce_sums(sum_heads(*x_mx[0])))]
+        x_of = {(0, 0): quantise_x(x_grouped[0])}
+        neg_means = {0: negate_means(reduce_sums(sum_heads(0, *x_of[0, 0])))}
+        x_of[0, 1] = quantise_x(x_grouped[1])
         ab_waiting = {1: multiply_ab(1, psum_c, "c1"), 2: multiply_ab(2, psum_c, "c0")}
 
         def kind_of(h):
@@ -283,7 +284,7 @@ def tile_gqa_flashattn_pa_t_kernel(
                     out=unread[:, h, :],
                     in_=head_of(banks, h),
                     func=ACT.Square,
-                    bias=neg_mean[:, t % 2, h : h + 1],
+                    bias=neg_mean[:, h : h + 1],
                     scale=1.0,
                     accum_out=sum_sq[:, h : h + 1],
                 )
@@ -292,7 +293,7 @@ def tile_gqa_flashattn_pa_t_kernel(
                     out=centred[:, t % 2, h - GP_HEADS[0], :],
                     in_=head_of(banks, h),
                     func=ACT.Identity,
-                    bias=neg_mean[:, t % 2, h : h + 1],
+                    bias=neg_mean[:, h : h + 1],
                     scale=1.0,
                 )
             v_sb = outs.tile([P, KV_HEADS, HD], F32)
@@ -316,7 +317,7 @@ def tile_gqa_flashattn_pa_t_kernel(
                 nc.vector.scalar_tensor_tensor(
                     out=pair_ab[:, t % 2, h, 0:tables, :],
                     in0=head_of(banks, h).unsqueeze(1).to_broadcast([P, tables, HD]),
-                    scalar=neg_mean[:, t % 2, h : h + 1],
+                    scalar=neg_mean[:, h : h + 1],
                     in1=tab_ab[:, t, 0:tables, kind_of(h), :],
                     op0=ADD,
                     op1=MULT,
@@ -358,10 +359,7 @@ def tile_gqa_flashattn_pa_t_kernel(
         c_ps = []
         waiting = []
         grouped = {}
-        sums = {}
         totals = {}
-        x_of = {(0, 0): x_mx[0], (0, 1): x_mx[1]}
-        mean_of = {(0, 0): neg_means[0]}
         for i in range(TILES):
             b, t = divmod(i, T)
             if t % 2 == 0:
@@ -370,35 +368,33 @@ def tile_gqa_flashattn_pa_t_kernel(
                 rotated = work.tile([P, 2, NORMED, HD], F32)
             banks = project(t, *x_of[b, t // 2])
             if i == 0:
-                sums[0, 1] = sum_heads(*x_of[0, 1])
+                totals[1] = reduce_sums(sum_heads(1, *x_of[0, 0]))
+                sums = [sum_heads(2, *x_of[0, 1])]
             if i == 1:
                 ab_waiting[3] = multiply_ab(3, psum_c, "c1")
             if i in (2, 3):
                 c_ps.append(multiply_c(i - 2))
-            if b + 1 < B and t >= 2:
-                sums[b + 1, t - 2] = sum_heads(*x_of[b + 1, t - 2])
-            rstd = measure(b, t, banks, mean_of[b, t // 2], centred)
+            ahead = i + LEAD
+            rstd = measure(b, t, banks, neg_means[i], centred)
+            if i + 1 in totals:
+                neg_means[i + 1] = negate_means(totals[i + 1])
             if i + 1 in ab_waiting:
                 copy_ab(i + 1, ab_waiting[i + 1])
             if b + 1 < B and t < 2:
                 grouped[b + 1, t] = transpose_x(b + 1, t)
-            products(t, banks, mean_of[b, t // 2], pair_ab)
+            products(t, banks, neg_means[i], pair_ab)
             if i == 0:
+                totals[2] = reduce_sums(sums[0])
                 diagonals_for_c(spread)
-                totals[0, 1] = reduce_sums(sums[0, 1])
+            if ahead < TILES:
+                totals[ahead] = reduce_sums(sum_heads(ahead % T, *x_of[ahead // T, ahead % T // 2]))
+            if b + 1 < B and t < 2:
+                x_of[b + 1, t] = quantise_x(grouped[b + 1, t])
             waiting.append((b, t, rotated, rstd))
             if t % 2 == 1:
                 rotate(t - 1, 2, pair_ab, centred, rotated)
             if len(waiting) > LAG:
                 finish(*waiting[0])
                 waiting = waiting[1:]
-            if b + 1 < B and t < 2:
-                x_of[b + 1, t] = quantise_x(grouped[b + 1, t])
-            if b + 1 < B and t >= 2:
-                totals[b + 1, t - 2] = reduce_sums(sums[b + 1, t - 2])
-            if b + 1 < B and t == 3:
-                mean_of[b + 1, 0] = negate_means(totals[b + 1, 0])
-            if t == (0 if b > 0 else 1):
-                mean_of[b, 1] = negate_means(totals[b, 1])
         for tile in waiting:
             finish(*tile)

@@ -30,7 +30,8 @@ RUNS = HD // RUN
 GP_HEADS = range(Q_HEADS, NORMED)
 TILES = B * T
 LAG = 3
-LEAD = 3
+PAIRS = TILES // 2
+W_LOAD = 256
 
 FLOPS = 2 * B * S * D * W_COLS
 
@@ -67,9 +68,10 @@ def tile_gqa_flashattn_pa_t_kernel(
         warm = const.tile([P, 1], F32)
         nc.scalar.activation(out=warm[:], in_=eps[:], func=ACT.Abs_reciprocal_sqrt)
 
-        def load_w(w, name):
-            raw = const.tile([P, PACK * w.shape[1]], BF16, name=name)
-            nc.sync.dma_start(out=raw[:], in_=w.rearrange("(p v) c -> p (v c)", v=PACK))
+        def load_w(w, name, first_col=0):
+            raw = const.tile([P, PACK, W_LOAD], BF16, name=name)
+            rows = w.rearrange("(p v) c -> p v c", v=PACK)
+            nc.sync.dma_start(out=raw[:], in_=rows[:, :, first_col : first_col + W_LOAD])
             return raw
 
         def load_x(b, pair):
@@ -79,14 +81,16 @@ def tile_gqa_flashattn_pa_t_kernel(
             )
             return x_sb
 
-        wq_raw = load_w(Wq, "wq_raw")
+        wq_raw = [load_w(Wq, "wq_raw%d" % n, n * W_LOAD) for n in range(2)]
+        wk_raw = load_w(Wk, "wk_raw")
+        wv_raw = load_w(Wv, "wv_raw")
+        x_pairs = [load_x(0, 0)]
         cos_sb = const.tile([P, T, HD], BF16)
         nc.sync.dma_start(out=cos_sb[:], in_=cos.rearrange("(p t) j -> p t j", t=T))
         sin_sb = const.tile([P, T, HD], BF16)
         nc.sync.dma_start(out=sin_sb[:], in_=sin.rearrange("(p t) j -> p t j", t=T))
-        wk_raw = load_w(Wk, "wk_raw")
-        wv_raw = load_w(Wv, "wv_raw")
-        x_tiles = [[load_x(b, pair) for pair in range(2)] for b in range(B)]
+        x_pairs.append(load_x(0, 1))
+        x_pairs.extend(load_x(b, pair) for b in range(1, B) for pair in range(2))
 
         signs = const.tile([P, 3, P], BF16)
         nc.vector.tensor_copy(out=signs[:, 0, :], in_=ident[:])
@@ -95,6 +99,14 @@ def tile_gqa_flashattn_pa_t_kernel(
         nc.vector.tensor_scalar_mul(out=signs[:, 1, HALF:HD], in0=ident[:, 0:HALF], scalar1=-1.0)
         nc.vector.tensor_scalar_mul(out=signs[:, 2, 0:HALF], in0=ident[:, 0:HALF], scalar1=-1.0)
         ident_b = signs[:, 0, :]
+        to_mean = const.tile([P, HEADS], F32)
+        nc.vector.tensor_reduce(
+            out=to_mean[:],
+            in_=ident[:].rearrange("p (h c) -> p h c", c=RUN),
+            axis=mybir.AxisListType.X,
+            op=ADD,
+        )
+        nc.vector.tensor_scalar_mul(out=to_mean[:], in0=to_mean[:], scalar1=-1.0 / HD)
 
         w_grouped = const.tile([P, W_COLS * PACK], BF16, align_bytes=64)
         w_codes = const.tile([P, W_COLS], U32, align_bytes=64)
@@ -103,12 +115,12 @@ def tile_gqa_flashattn_pa_t_kernel(
         m_codes = const.tile([P, W_COLS], U32, align_bytes=64)
         m_scales = const.tile([P, W_COLS], U8, align_bytes=64)
 
-        def regroup_w(copy, raw, first_col, cols):
+        def regroup_w(copy, raw, first_col):
             copy(
-                out=w_grouped[:, first_col * PACK : (first_col + cols) * PACK].rearrange(
+                out=w_grouped[:, first_col * PACK : (first_col + W_LOAD) * PACK].rearrange(
                     "p (c v) -> p c v", v=PACK
                 ),
-                in_=raw[:].rearrange("p (v c) -> p c v", v=PACK),
+                in_=raw[:].rearrange("p v c -> p c v"),
             )
 
         def quantise_w(first_col, cols):
@@ -118,9 +130,9 @@ def tile_gqa_flashattn_pa_t_kernel(
                 in_=w_grouped[:, first_col * PACK : (first_col + cols) * PACK],
             )
 
-        def transpose_x(b, pair):
-            x_words = x_tiles[b][pair][:].bitcast(F32)
-            x_t = psum_x.tile([P, BANK], F32, tag="x_t")
+        def transpose_x(pair):
+            x_words = x_pairs[pair][:].bitcast(F32)
+            x_t = psum_x.tile([P, BANK], F32, tag="x", name="x_t")
             for n in range(BANK // P):
                 first = (n // 2) * 2 * P + n % 2
                 nc.tensor.transpose(
@@ -128,45 +140,59 @@ def tile_gqa_flashattn_pa_t_kernel(
                     x_words[:, first : first + 2 * P - 1 : 2],
                     ident[:],
                 )
+            return x_t
+
+        def group_x(copy, x_t):
             grouped = xprep.tile([P, 2 * P * PACK], BF16, align_bytes=64)
-            nc.scalar.copy(
+            copy(
                 out=grouped[:].bitcast(F32).rearrange("p (t r u) -> p t r u", t=2, u=2),
                 in_=x_t[:].rearrange("p (t u r) -> p t r u", t=2, u=2),
             )
             return grouped
 
-        def quantise_x(grouped):
+        x_mx = {}
+
+        def quantise_x(pair, grouped):
             codes = xprep.tile([P, 2 * P], U32, align_bytes=64)
             scales = xprep.tile([P, 2 * P], U8, align_bytes=64)
             nc.vector.quantize_mx(out=codes[:].bitcast(FP8X4), scales=scales[:], in_=grouped[:])
-            return codes, scales
+            x_mx[pair] = codes, scales
 
-        def sum_heads(t, codes, scales):
-            sums = psum_m.tile([P, HEADS, RUN], F32, tag="mean")
-            token_cols = slice(t % 2 * P, (t % 2 + 1) * P)
-            for i in range(RUNS):
+        sums = {}
+
+        def add_runs(pair, runs):
+            if runs[0] == 0:
+                sums[pair] = psum_m.tile([P, 2 * P], F32, tag="sums", name="sums")
+            codes, scales = x_mx[pair]
+            for i in runs:
                 cols = slice(i * P, (i + 1) * P)
                 nc.tensor.matmul_mx(
-                    out=sums[:].rearrange("p h c -> p (h c)"),
-                    lhsT=codes[:, token_cols].bitcast(FP8X4),
-                    lhsT_scale=scales[:, token_cols],
-                    rhs=m_codes[:, cols].bitcast(FP8X4),
-                    rhs_scale=m_scales[:, cols],
+                    out=sums[pair][:],
+                    lhsT=m_codes[:, cols].bitcast(FP8X4),
+                    lhsT_scale=m_scales[:, cols],
+                    rhs=codes[:].bitcast(FP8X4),
+                    rhs_scale=scales[:],
                     start=i == 0,
                     stop=i == RUNS - 1,
                 )
-            return sums
 
-        def reduce_sums(sums):
-            total = stats.tile([P, NORMED], F32)
-            nc.vector.tensor_reduce(
-                out=total[:], in_=sums[:, 0:NORMED, :], axis=mybir.AxisListType.X, op=ADD
-            )
-            return total
+        def keep_sums(pair):
+            sums_sb = stats.tile([P, 2 * P], F32)
+            nc.scalar.copy(out=sums_sb[:], in_=sums[pair][:])
+            return sums_sb
 
-        def negate_means(total):
-            neg_mean = stats.tile([P, NORMED], F32)
-            nc.scalar.mul(out=neg_mean[:], in_=total[:], mul=-1.0 / HD)
+        def make_means(sums_sb):
+            means = psum_x.tile([P, 2, HEADS], F32, tag="x", name="means")
+            for t in range(2):
+                nc.tensor.matmul(
+                    out=means[:, t, :],
+                    lhsT=sums_sb[:, t * P : (t + 1) * P],
+                    rhs=to_mean[:],
+                    start=True,
+                    stop=True,
+                )
+            neg_mean = stats.tile([P, 2, HEADS], F32)
+            nc.scalar.copy(out=neg_mean[:], in_=means[:])
             return neg_mean
 
         diag = const.tile([P, 4, 2, HD], BF16)
@@ -185,8 +211,8 @@ def tile_gqa_flashattn_pa_t_kernel(
                 )
             return ab
 
-        def copy_ab(t, ab):
-            nc.scalar.copy(
+        def copy_ab(copy, t, ab):
+            copy(
                 out=tab_ab[:, t].rearrange("p n k j -> p (n k j)"),
                 in_=ab[:].rearrange("p n c -> p (n c)"),
             )
@@ -223,34 +249,35 @@ def tile_gqa_flashattn_pa_t_kernel(
         nc.tensor.matmul(
             out=spread[:].rearrange("p n j -> p (n j)"), lhsT=ones[:], rhs=vecs[:], start=True, stop=True
         )
-        trig_t = psum_u.tile([P, 2, T, P], BF16, tag="u_q")
-        for n, table in enumerate((cos_sb, sin_sb)):
-            for t in range(T):
-                nc.tensor.transpose(trig_t[:, n, t, :], table[:, t, :], ident_b)
-        regroup_w(nc.vector.tensor_copy, wq_raw, 0, BANK)
-        nc.scalar.copy(out=trig[:], in_=trig_t[:])
-        nc.vector.tensor_tensor(
-            out=diag[:, 0:2],
-            in0=signs[:, 0:2, :].unsqueeze(2).to_broadcast([P, 2, 2, HD]),
-            in1=spread[:, 0:2, :].unsqueeze(1).to_broadcast([P, 2, 2, HD]),
-            op=MULT,
-        )
-        regroup_w(nc.scalar.copy, wk_raw, BANK, KV_HEADS * HD)
+        regroup_w(nc.vector.tensor_copy, wq_raw[0], 0)
+        regroup_w(nc.vector.tensor_copy, wq_raw[1], W_LOAD)
+        regroup_w(nc.scalar.copy, wk_raw, BANK)
         quantise_w(0, BANK)
-        regroup_w(nc.vector.tensor_copy, wv_raw, BANK + KV_HEADS * HD, KV_HEADS * HD)
-        x_grouped = [transpose_x(0, 0)]
-        copy_ab(0, multiply_ab(0, psum_u, "u_q"))
+        regroup_w(nc.vector.tensor_copy, wv_raw, BANK + W_LOAD)
+        x_grouped = group_x(nc.scalar.copy, transpose_x(0))
         quantise_w(BANK, BANK)
         for dst, src, per_run in ((m_codes, w_codes, RUN), (m_scales, w_scales, RUN // PACK)):
             nc.vector.tensor_copy(
                 out=dst[:].bitcast(I32).rearrange("p (i h c) -> p h i c", h=HEADS, c=per_run),
                 in_=src[:].bitcast(I32).rearrange("p (h i c) -> p h i c", h=HEADS, c=per_run),
             )
-        x_grouped.append(transpose_x(0, 1))
-        x_of = {(0, 0): quantise_x(x_grouped[0])}
-        neg_means = {0: negate_means(reduce_sums(sum_heads(0, *x_of[0, 0])))}
-        x_of[0, 1] = quantise_x(x_grouped[1])
-        ab_waiting = {1: multiply_ab(1, psum_c, "c1"), 2: multiply_ab(2, psum_c, "c0")}
+        quantise_x(0, x_grouped)
+        trig_t = psum_u.tile([P, 2, T, P], BF16, tag="u_q")
+        for n, table in enumerate((cos_sb, sin_sb)):
+            for t in range(T):
+                nc.tensor.transpose(trig_t[:, n, t, :], table[:, t, :], ident_b)
+        nc.scalar.copy(out=trig[:], in_=trig_t[:])
+        x_grouped = group_x(nc.scalar.copy, transpose_x(1))
+        nc.vector.tensor_tensor(
+            out=diag[:, 0:2],
+            in0=signs[:, 0:2, :].unsqueeze(2).to_broadcast([P, 2, 2, HD]),
+            in1=spread[:, 0:2, :].unsqueeze(1).to_broadcast([P, 2, 2, HD]),
+            op=MULT,
+        )
+        add_runs(0, range(RUNS))
+        copy_ab(nc.vector.tensor_copy, 0, multiply_ab(0, psum_u, "u_q"))
+        quantise_x(1, x_grouped)
+        diagonals_for_c(spread)
 
         def kind_of(h):
             return 0 if h < Q_HEADS else 1
@@ -276,7 +303,7 @@ def tile_gqa_flashattn_pa_t_kernel(
             col = (h % Q_HEADS) * HD
             return banks[kind_of(h)][:, col : col + HD]
 
-        def measure(b, t, banks, neg_mean, centred):
+        def measure(b, t, banks, neg_mean, centred, gp_heads):
             sum_sq = stats.tile([P, NORMED], F32)
             unread = work.tile([P, NORMED, HD], BF16)
             for h in range(NORMED):
@@ -284,16 +311,16 @@ def tile_gqa_flashattn_pa_t_kernel(
                     out=unread[:, h, :],
                     in_=head_of(banks, h),
                     func=ACT.Square,
-                    bias=neg_mean[:, h : h + 1],
+                    bias=neg_mean[:, t % 2, h : h + 1],
                     scale=1.0,
                     accum_out=sum_sq[:, h : h + 1],
                 )
-            for h in GP_HEADS:
+            for h in gp_heads:
                 nc.scalar.activation(
                     out=centred[:, t % 2, h - GP_HEADS[0], :],
                     in_=head_of(banks, h),
                     func=ACT.Identity,
-                    bias=neg_mean[:, h : h + 1],
+                    bias=neg_mean[:, t % 2, h : h + 1],
                     scale=1.0,
                 )
             v_sb = outs.tile([P, KV_HEADS, HD], F32)
@@ -311,13 +338,13 @@ def tile_gqa_flashattn_pa_t_kernel(
             )
             return rstd
 
-        def products(t, banks, neg_mean, pair_ab):
+        def products(t, banks, neg_mean, pair_ab, gp_heads):
             for h in range(NORMED):
-                tables = 1 if h in GP_HEADS else 2
+                tables = 1 if h in gp_heads else 2
                 nc.vector.scalar_tensor_tensor(
                     out=pair_ab[:, t % 2, h, 0:tables, :],
                     in0=head_of(banks, h).unsqueeze(1).to_broadcast([P, tables, HD]),
-                    scalar=neg_mean[:, h : h + 1],
+                    scalar=neg_mean[:, t % 2, h : h + 1],
                     in1=tab_ab[:, t, 0:tables, kind_of(h), :],
                     op0=ADD,
                     op1=MULT,
@@ -333,10 +360,13 @@ def tile_gqa_flashattn_pa_t_kernel(
                 in1=tab_ab[:, t0 : t0 + count, 1, 1:2, :].to_broadcast([P, count, heads, HD]),
                 op=MULT,
             )
-            pair = pair_ab[:, mine].rearrange("p t h n j -> p (t h) n j")
-            out = rotated[:, mine].rearrange("p t h j -> p (t h) j")
+            add_turned(nc.gpsimd, pair_ab[:, mine], rotated[:, mine])
+
+        def add_turned(engine, pair_ab, rotated):
+            pair = pair_ab.rearrange("p t h n j -> p (t h) n j")
+            out = rotated.rearrange("p t h j -> p (t h) j")
             for to, other in ((slice(0, HALF), slice(HALF, HD)), (slice(HALF, HD), slice(0, HALF))):
-                nc.gpsimd.tensor_tensor(
+                engine.tensor_tensor(
                     out=out[:, :, to], in0=pair[:, :, 0, to], in1=pair[:, :, 1, other], op=ADD
                 )
 
@@ -358,43 +388,51 @@ def tile_gqa_flashattn_pa_t_kernel(
 
         c_ps = []
         waiting = []
-        grouped = {}
-        totals = {}
+        banks = {0: project(0, *x_mx[0])}
+        neg_means = {0: make_means(keep_sums(0))}
+        copy_ab(nc.vector.tensor_copy, 1, multiply_ab(1, psum_c, "c1"))
+        banks[1] = project(1, *x_mx[0])
+        add_runs(1, range(RUNS // 2))
         for i in range(TILES):
             b, t = divmod(i, T)
-            if t % 2 == 0:
+            pair, side = divmod(i, 2)
+            if side == 0:
                 pair_ab = work.tile([P, 2, NORMED, 2, HD], F32)
                 centred = work.tile([P, 2, len(GP_HEADS), HD], F32)
                 rotated = work.tile([P, 2, NORMED, HD], F32)
-            banks = project(t, *x_of[b, t // 2])
+            if i > 1:
+                banks[i] = project(t, *x_mx[pair])
+            gp_heads = GP_HEADS if i < TILES - 1 else ()
+            rstd = measure(b, t, banks[i], neg_means[pair], centred, gp_heads)
+            products(t, banks[i], neg_means[pair], pair_ab, gp_heads)
+            waiting.append((b, t, rotated, rstd))
+
             if i == 0:
-                totals[1] = reduce_sums(sum_heads(1, *x_of[0, 0]))
-                sums = [sum_heads(2, *x_of[0, 1])]
+                copy_ab(nc.vector.tensor_copy, 2, multiply_ab(2, psum_c, "c0"))
+                ab_3 = multiply_ab(3, psum_c, "c1")
             if i == 1:
-                ab_waiting[3] = multiply_ab(3, psum_c, "c1")
+                copy_ab(nc.vector.tensor_copy, 3, ab_3)
             if i in (2, 3):
                 c_ps.append(multiply_c(i - 2))
-            ahead = i + LEAD
-            rstd = measure(b, t, banks, neg_means[i], centred)
-            if i + 1 in totals:
-                neg_means[i + 1] = negate_means(totals[i + 1])
-            if i + 1 in ab_waiting:
-                copy_ab(i + 1, ab_waiting[i + 1])
-            if b + 1 < B and t < 2:
-                grouped[b + 1, t] = transpose_x(b + 1, t)
-            products(t, banks, neg_means[i], pair_ab)
-            if i == 0:
-                totals[2] = reduce_sums(sums[0])
-                diagonals_for_c(spread)
-            if ahead < TILES:
-                totals[ahead] = reduce_sums(sum_heads(ahead % T, *x_of[ahead // T, ahead % T // 2]))
-            if b + 1 < B and t < 2:
-                x_of[b + 1, t] = quantise_x(grouped[b + 1, t])
-            waiting.append((b, t, rotated, rstd))
-            if t % 2 == 1:
+
+            if side == 0 and pair + 1 < PAIRS:
+                add_runs(pair + 1, range(RUNS // 2, RUNS))
+                sums_sb = keep_sums(pair + 1)
+                if pair + 2 < PAIRS:
+                    copy = nc.scalar.copy if i > 0 else nc.vector.tensor_copy
+                    quantise_x(pair + 2, group_x(copy, transpose_x(pair + 2)))
+            if side == 1 and pair + 1 < PAIRS:
+                neg_means[pair + 1] = make_means(sums_sb)
+                if pair + 2 < PAIRS:
+                    add_runs(pair + 2, range(RUNS // 2))
+
+            if i < 2 or TILES - 4 <= i < TILES - 1:
+                rotate(t, 1, pair_ab, centred, rotated)
+            elif side == 1 and i < TILES - 1:
                 rotate(t - 1, 2, pair_ab, centred, rotated)
-            if len(waiting) > LAG:
+            while len(waiting) > (LAG if i < TILES - 2 else LAG - 1):
                 finish(*waiting[0])
                 waiting = waiting[1:]
+        add_turned(nc.vector, pair_ab[:, 1:2], rotated[:, 1:2])
         for tile in waiting:
             finish(*tile)

@@ -27,11 +27,13 @@ W_COLS = (Q_HEADS + 2 * KV_HEADS) * HD
 EPS = 1e-6
 HEADS = Q_HEADS + 2 * KV_HEADS
 RUNS = HD // RUN
-GP_HEADS = range(Q_HEADS, NORMED)
+GP_HEADS = range(2, Q_HEADS)
 TILES = B * T
+SHARED = range(4, TILES - 1)
 LAG = 3
 PAIRS = TILES // 2
 W_LOAD = 256
+ORDER = (*range(Q_HEADS, NORMED), *range(Q_HEADS))
 
 FLOPS = 2 * B * S * D * W_COLS
 
@@ -45,7 +47,7 @@ def tile_gqa_flashattn_pa_t_kernel(
         xprep = ctx.enter_context(tc.tile_pool(name="xprep", bufs=4))
         stats = ctx.enter_context(tc.tile_pool(name="stats", bufs=8))
         work = ctx.enter_context(tc.tile_pool(name="work", bufs=3))
-        outs = ctx.enter_context(tc.tile_pool(name="outs", bufs=4))
+        outs = ctx.enter_context(tc.tile_pool(name="outs", bufs=8))
         psum_c = ctx.enter_context(tc.psum_pool(name="psum_c", bufs=1))
         psum_x = ctx.enter_context(tc.psum_pool(name="psum_x", bufs=1))
         psum_m = ctx.enter_context(tc.psum_pool(name="psum_m", bufs=1))
@@ -256,28 +258,24 @@ def tile_gqa_flashattn_pa_t_kernel(
         regroup_w(nc.vector.tensor_copy, wv_raw, BANK + W_LOAD)
         x_grouped = group_x(nc.scalar.copy, transpose_x(0))
         quantise_w(BANK, BANK)
-        for dst, src, per_run in ((m_codes, w_codes, RUN), (m_scales, w_scales, RUN // PACK)):
-            nc.vector.tensor_copy(
-                out=dst[:].bitcast(I32).rearrange("p (i h c) -> p h i c", h=HEADS, c=per_run),
-                in_=src[:].bitcast(I32).rearrange("p (h i c) -> p h i c", h=HEADS, c=per_run),
-            )
         quantise_x(0, x_grouped)
-        trig_t = psum_u.tile([P, 2, T, P], BF16, tag="u_q")
+        trig_t = psum_m.tile([P, 2, T, P], BF16, tag="sums")
         for n, table in enumerate((cos_sb, sin_sb)):
             for t in range(T):
                 nc.tensor.transpose(trig_t[:, n, t, :], table[:, t, :], ident_b)
         nc.scalar.copy(out=trig[:], in_=trig_t[:])
-        x_grouped = group_x(nc.scalar.copy, transpose_x(1))
         nc.vector.tensor_tensor(
             out=diag[:, 0:2],
             in0=signs[:, 0:2, :].unsqueeze(2).to_broadcast([P, 2, 2, HD]),
             in1=spread[:, 0:2, :].unsqueeze(1).to_broadcast([P, 2, 2, HD]),
             op=MULT,
         )
-        add_runs(0, range(RUNS))
-        copy_ab(nc.vector.tensor_copy, 0, multiply_ab(0, psum_u, "u_q"))
-        quantise_x(1, x_grouped)
         diagonals_for_c(spread)
+        for dst, src, per_run in ((m_codes, w_codes, RUN), (m_scales, w_scales, RUN // PACK)):
+            nc.vector.tensor_copy(
+                out=dst[:].bitcast(I32).rearrange("p (i h c) -> p h i c", h=HEADS, c=per_run),
+                in_=src[:].bitcast(I32).rearrange("p (h i c) -> p h i c", h=HEADS, c=per_run),
+            )
 
         def kind_of(h):
             return 0 if h < Q_HEADS else 1
@@ -303,10 +301,23 @@ def tile_gqa_flashattn_pa_t_kernel(
             col = (h % Q_HEADS) * HD
             return banks[kind_of(h)][:, col : col + HD]
 
+        def means_by_scalar(banks):
+            neg_mean = stats.tile([P, 2, HEADS], F32)
+            unread = work.tile([P, NORMED, HD], BF16)
+            for h in ORDER:
+                nc.scalar.activation(
+                    out=unread[:, h, :],
+                    in_=head_of(banks, h),
+                    func=ACT.Copy,
+                    scale=-1.0 / HD,
+                    accum_out=neg_mean[:, 0, h : h + 1],
+                )
+            return neg_mean
+
         def measure(b, t, banks, neg_mean, centred, gp_heads):
             sum_sq = stats.tile([P, NORMED], F32)
             unread = work.tile([P, NORMED, HD], BF16)
-            for h in range(NORMED):
+            for h in ORDER:
                 nc.scalar.activation(
                     out=unread[:, h, :],
                     in_=head_of(banks, h),
@@ -315,19 +326,23 @@ def tile_gqa_flashattn_pa_t_kernel(
                     scale=1.0,
                     accum_out=sum_sq[:, h : h + 1],
                 )
+                if h == NORMED - 1:
+                    v_sb = outs.tile([P, KV_HEADS, HD], F32)
+                    nc.scalar.copy(
+                        out=v_sb[:].rearrange("p h j -> p (h j)"),
+                        in_=banks[1][:, KV_HEADS * HD : BANK],
+                    )
+                    nc.sync.dma_start(
+                        out=out_2[b].rearrange("h (p t) j -> t p h j", t=T)[t], in_=v_sb[:]
+                    )
             for h in gp_heads:
                 nc.scalar.activation(
-                    out=centred[:, t % 2, h - GP_HEADS[0], :],
+                    out=centred[:, t % 2, h, :],
                     in_=head_of(banks, h),
                     func=ACT.Identity,
                     bias=neg_mean[:, t % 2, h : h + 1],
                     scale=1.0,
                 )
-            v_sb = outs.tile([P, KV_HEADS, HD], F32)
-            nc.scalar.copy(
-                out=v_sb[:].rearrange("p h j -> p (h j)"), in_=banks[1][:, KV_HEADS * HD : BANK]
-            )
-            nc.sync.dma_start(out=out_2[b].rearrange("h (p t) j -> t p h j", t=T)[t], in_=v_sb[:])
             rstd = stats.tile([P, NORMED], F32)
             nc.scalar.activation(
                 out=rstd[:],
@@ -339,7 +354,7 @@ def tile_gqa_flashattn_pa_t_kernel(
             return rstd
 
         def products(t, banks, neg_mean, pair_ab, gp_heads):
-            for h in range(NORMED):
+            for h in ORDER:
                 tables = 1 if h in gp_heads else 2
                 nc.vector.scalar_tensor_tensor(
                     out=pair_ab[:, t % 2, h, 0:tables, :],
@@ -350,89 +365,117 @@ def tile_gqa_flashattn_pa_t_kernel(
                     op1=MULT,
                 )
 
-        def rotate(t0, count, pair_ab, centred, rotated):
-            first = t0 % 2
-            mine = slice(first, first + count)
-            heads = len(GP_HEADS)
+        def multiply_b(t0, count, pair_ab, centred, gp_heads):
+            mine = slice(t0 % 2, t0 % 2 + count)
+            heads = len(gp_heads)
             nc.gpsimd.tensor_tensor(
-                out=pair_ab[:, mine, GP_HEADS[0] :, 1, :],
-                in0=centred[:, mine],
-                in1=tab_ab[:, t0 : t0 + count, 1, 1:2, :].to_broadcast([P, count, heads, HD]),
+                out=pair_ab[:, mine, gp_heads[0] : Q_HEADS, 1, :],
+                in0=centred[:, mine, gp_heads[0] : Q_HEADS],
+                in1=tab_ab[:, t0 : t0 + count, 1, 0:1, :].to_broadcast([P, count, heads, HD]),
                 op=MULT,
             )
-            add_turned(nc.gpsimd, pair_ab[:, mine], rotated[:, mine])
 
-        def add_turned(engine, pair_ab, rotated):
-            pair = pair_ab.rearrange("p t h n j -> p (t h) n j")
-            out = rotated.rearrange("p t h j -> p (t h) j")
-            for to, other in ((slice(0, HALF), slice(HALF, HD)), (slice(HALF, HD), slice(0, HALF))):
-                engine.tensor_tensor(
-                    out=out[:, :, to], in0=pair[:, :, 0, to], in1=pair[:, :, 1, other], op=ADD
-                )
+        def add_turned(engine, out, ab):
+            halves = ab.rearrange("p n k (u j) -> p n k u j", u=2)
+            engine.tensor_tensor(
+                out=out.rearrange("p n (u j) -> p n u j", u=2),
+                in0=halves[:, :, 0],
+                in1=halves[:, :, 1, ::-1],
+                op=ADD,
+            )
 
-        def finish(b, t, rotated, rstd):
+        def finish(i, rotated, rstd):
+            b, t = divmod(i, T)
             q_sb = outs.tile([P, Q_HEADS, HD], F32)
             k_sb = outs.tile([P, KV_HEADS, HD], F32)
             for h in range(NORMED):
-                dst = q_sb[:, h, :] if h < Q_HEADS else k_sb[:, h - Q_HEADS, :]
                 nc.vector.scalar_tensor_tensor(
-                    out=dst,
+                    out=q_sb[:, h, :] if h < Q_HEADS else k_sb[:, h - Q_HEADS, :],
                     in0=rotated[:, t % 2, h, :],
                     scalar=rstd[:, h : h + 1],
                     in1=c_ps[t // 2][:, t % 2, kind_of(h), :],
                     op0=MULT,
                     op1=ADD,
                 )
-            nc.sync.dma_start(out=out_0[b].rearrange("h (p t) j -> t p h j", t=T)[t], in_=q_sb[:])
+                if h == Q_HEADS - 1:
+                    nc.sync.dma_start(
+                        out=out_0[b].rearrange("h (p t) j -> t p h j", t=T)[t], in_=q_sb[:]
+                    )
             nc.sync.dma_start(out=out_1[b].rearrange("h (p t) j -> t p h j", t=T)[t], in_=k_sb[:])
 
         c_ps = []
         waiting = []
         banks = {0: project(0, *x_mx[0])}
-        neg_means = {0: make_means(keep_sums(0))}
-        copy_ab(nc.vector.tensor_copy, 1, multiply_ab(1, psum_c, "c1"))
+        neg_means = {0: means_by_scalar(banks[0])}
+        quantise_x(1, group_x(nc.vector.tensor_copy, transpose_x(1)))
+        copy_ab(nc.vector.tensor_copy, 0, multiply_ab(0, psum_c, "c0"))
+        add_runs(0, range(RUNS))
+        ab_1, ab_2 = multiply_ab(1, psum_c, "c1"), multiply_ab(2, psum_c, "c0")
         banks[1] = project(1, *x_mx[0])
-        add_runs(1, range(RUNS // 2))
         for i in range(TILES):
             b, t = divmod(i, T)
             pair, side = divmod(i, 2)
             if side == 0:
                 pair_ab = work.tile([P, 2, NORMED, 2, HD], F32)
-                centred = work.tile([P, 2, len(GP_HEADS), HD], F32)
+                centred = work.tile([P, 2, Q_HEADS, HD], F32)
                 rotated = work.tile([P, 2, NORMED, HD], F32)
-            if i > 1:
+            if i > 2:
                 banks[i] = project(t, *x_mx[pair])
-            gp_heads = GP_HEADS if i < TILES - 1 else ()
-            rstd = measure(b, t, banks[i], neg_means[pair], centred, gp_heads)
-            products(t, banks[i], neg_means[pair], pair_ab, gp_heads)
-            waiting.append((b, t, rotated, rstd))
+            gp_heads = range(GP_HEADS[0] - (pair % 3 == 0), Q_HEADS) if i in SHARED else ()
+            rstd = measure(b, t, banks[i], neg_means[i], centred, gp_heads)
+            if i == 0:
+                sums_sb = keep_sums(0)
 
             if i == 0:
-                copy_ab(nc.vector.tensor_copy, 2, multiply_ab(2, psum_c, "c0"))
-                ab_3 = multiply_ab(3, psum_c, "c1")
+                products(t, banks[0], neg_means[0], pair_ab, gp_heads)
+                copy_ab(nc.scalar.copy, 1, ab_1)
+                neg_means[1] = make_means(sums_sb)
+                add_runs(1, range(RUNS // 2))
+
             if i == 1:
-                copy_ab(nc.vector.tensor_copy, 3, ab_3)
+                banks[2] = project(2, *x_mx[1])
+                ab_3 = multiply_ab(3, psum_c, "c1")
             if i in (2, 3):
                 c_ps.append(multiply_c(i - 2))
 
             if side == 0 and pair + 1 < PAIRS:
                 add_runs(pair + 1, range(RUNS // 2, RUNS))
+            if pair + 1 < PAIRS and i in (1, *range(2, TILES, 2)):
                 sums_sb = keep_sums(pair + 1)
-                if pair + 2 < PAIRS:
-                    copy = nc.scalar.copy if i > 0 else nc.vector.tensor_copy
-                    quantise_x(pair + 2, group_x(copy, transpose_x(pair + 2)))
+            if i == 1:
+                copy_ab(nc.scalar.copy, 2, ab_2)
             if side == 1 and pair + 1 < PAIRS:
-                neg_means[pair + 1] = make_means(sums_sb)
-                if pair + 2 < PAIRS:
-                    add_runs(pair + 2, range(RUNS // 2))
+                neg_means[i + 1] = neg_means[i + 2] = make_means(sums_sb)
+            if i == 1:
+                copy_ab(nc.scalar.copy, 3, ab_3)
+            if side == 0 and pair + 2 < PAIRS:
+                x_t = transpose_x(pair + 2)
+                if i > 0:
+                    x_grouped = group_x(nc.scalar.copy, x_t)
+            if side == 1 and pair + 2 < PAIRS:
+                add_runs(pair + 2, range(RUNS // 2))
 
-            if i < 2 or TILES - 4 <= i < TILES - 1:
-                rotate(t, 1, pair_ab, centred, rotated)
-            elif side == 1 and i < TILES - 1:
-                rotate(t - 1, 2, pair_ab, centred, rotated)
+            if i > 0:
+                products(t, banks[i], neg_means[i], pair_ab, gp_heads)
+            waiting.append((i, rotated, rstd))
+            if i == 0:
+                x_grouped = group_x(nc.vector.tensor_copy, x_t)
+            if side == 0 and pair + 2 < PAIRS:
+                quantise_x(pair + 2, x_grouped)
+
+            single = i < 2 or TILES - 4 <= i < TILES - 1
+            if single or (side == 1 and i < TILES - 1):
+                mine = slice(side, side + 1) if single else slice(0, 2)
+                if gp_heads:
+                    multiply_b(t if single else t - 1, mine.stop - mine.start, pair_ab, centred, gp_heads)
+                add_turned(
+                    nc.gpsimd,
+                    rotated[:, mine].rearrange("p t h j -> p (t h) j"),
+                    pair_ab[:, mine].rearrange("p t h n j -> p (t h) n j"),
+                )
             while len(waiting) > (LAG if i < TILES - 2 else LAG - 1):
                 finish(*waiting[0])
                 waiting = waiting[1:]
-        add_turned(nc.vector, pair_ab[:, 1:2], rotated[:, 1:2])
+        add_turned(nc.vector, rotated[:, 1], pair_ab[:, 1])
         for tile in waiting:
             finish(*tile)

@@ -27,7 +27,7 @@ W_COLS = (Q_HEADS + 2 * KV_HEADS) * HD
 EPS = 1e-6
 HEADS = Q_HEADS + 2 * KV_HEADS
 RUNS = HD // RUN
-GP_HEADS = range(2, Q_HEADS)
+GP_HEADS = range(3, Q_HEADS)
 TILES = B * T
 SHARED = range(4, TILES - 1)
 LAG = 3
@@ -44,7 +44,7 @@ def tile_gqa_flashattn_pa_t_kernel(
     nc = tc.nc
     with ExitStack() as ctx:
         const = ctx.enter_context(tc.tile_pool(name="const", bufs=1))
-        xprep = ctx.enter_context(tc.tile_pool(name="xprep", bufs=4))
+        xprep = ctx.enter_context(tc.tile_pool(name="xprep", bufs=6))
         stats = ctx.enter_context(tc.tile_pool(name="stats", bufs=8))
         work = ctx.enter_context(tc.tile_pool(name="work", bufs=3))
         outs = ctx.enter_context(tc.tile_pool(name="outs", bufs=8))
@@ -62,11 +62,6 @@ def tile_gqa_flashattn_pa_t_kernel(
         nc.vector.memset(ones[:], 1.0)
         ident = const.tile([P, P], F32)
         make_identity(nc, ident[:])
-        for n, vec in enumerate((q_gamma, k_gamma, q_beta, k_beta)):
-            nc.scalar.dma_start(
-                out=vecs[0:1, n * HD : (n + 1) * HD], in_=vec.rearrange("(o j) -> o j", o=1)
-            )
-
         warm = const.tile([P, 1], F32)
         nc.scalar.activation(out=warm[:], in_=eps[:], func=ACT.Abs_reciprocal_sqrt)
 
@@ -83,7 +78,12 @@ def tile_gqa_flashattn_pa_t_kernel(
             )
             return x_sb
 
-        wq_raw = [load_w(Wq, "wq_raw%d" % n, n * W_LOAD) for n in range(2)]
+        wq_raw = [load_w(Wq, "wq_raw0")]
+        for n, vec in enumerate((q_gamma, k_gamma, q_beta, k_beta)):
+            nc.sync.dma_start(
+                out=vecs[0:1, n * HD : (n + 1) * HD], in_=vec.rearrange("(o j) -> o j", o=1)
+            )
+        wq_raw.append(load_w(Wq, "wq_raw1", W_LOAD))
         wk_raw = load_w(Wk, "wk_raw")
         wv_raw = load_w(Wv, "wv_raw")
         x_pairs = [load_x(0, 0)]
@@ -183,8 +183,8 @@ def tile_gqa_flashattn_pa_t_kernel(
             nc.scalar.copy(out=sums_sb[:], in_=sums[pair][:])
             return sums_sb
 
-        def make_means(sums_sb):
-            means = psum_x.tile([P, 2, HEADS], F32, tag="x", name="means")
+        def make_means(sums_sb, pool, tag):
+            means = pool.tile([P, 2, HEADS], F32, tag=tag, name="means")
             for t in range(2):
                 nc.tensor.matmul(
                     out=means[:, t, :],
@@ -253,17 +253,6 @@ def tile_gqa_flashattn_pa_t_kernel(
         )
         regroup_w(nc.vector.tensor_copy, wq_raw[0], 0)
         regroup_w(nc.vector.tensor_copy, wq_raw[1], W_LOAD)
-        regroup_w(nc.scalar.copy, wk_raw, BANK)
-        quantise_w(0, BANK)
-        regroup_w(nc.vector.tensor_copy, wv_raw, BANK + W_LOAD)
-        x_grouped = group_x(nc.scalar.copy, transpose_x(0))
-        quantise_w(BANK, BANK)
-        quantise_x(0, x_grouped)
-        trig_t = psum_m.tile([P, 2, T, P], BF16, tag="sums")
-        for n, table in enumerate((cos_sb, sin_sb)):
-            for t in range(T):
-                nc.tensor.transpose(trig_t[:, n, t, :], table[:, t, :], ident_b)
-        nc.scalar.copy(out=trig[:], in_=trig_t[:])
         nc.vector.tensor_tensor(
             out=diag[:, 0:2],
             in0=signs[:, 0:2, :].unsqueeze(2).to_broadcast([P, 2, 2, HD]),
@@ -271,6 +260,18 @@ def tile_gqa_flashattn_pa_t_kernel(
             op=MULT,
         )
         diagonals_for_c(spread)
+        regroup_w(nc.scalar.copy, wk_raw, BANK)
+        quantise_w(0, BANK)
+        regroup_w(nc.vector.tensor_copy, wv_raw, BANK + W_LOAD)
+        x_grouped = group_x(nc.scalar.copy, transpose_x(0))
+        quantise_w(BANK, BANK)
+        quantise_x(0, x_grouped)
+        x_t = transpose_x(1)
+        trig_t = psum_m.tile([P, 2, T, P], BF16, tag="sums")
+        for n, table in enumerate((cos_sb, sin_sb)):
+            for t in range(T):
+                nc.tensor.transpose(trig_t[:, n, t, :], table[:, t, :], ident_b)
+        nc.scalar.copy(out=trig[:], in_=trig_t[:])
         for dst, src, per_run in ((m_codes, w_codes, RUN), (m_scales, w_scales, RUN // PACK)):
             nc.vector.tensor_copy(
                 out=dst[:].bitcast(I32).rearrange("p (i h c) -> p h i c", h=HEADS, c=per_run),
@@ -353,9 +354,11 @@ def tile_gqa_flashattn_pa_t_kernel(
             )
             return rstd
 
-        def products(t, banks, neg_mean, pair_ab, gp_heads):
+        def products(t, banks, neg_mean, pair_ab, gp_heads, before_last=None):
             for h in ORDER:
                 tables = 1 if h in gp_heads else 2
+                if h == ORDER[-1] and before_last is not None:
+                    quantise_x(*before_last)
                 nc.vector.scalar_tensor_tensor(
                     out=pair_ab[:, t % 2, h, 0:tables, :],
                     in0=head_of(banks, h).unsqueeze(1).to_broadcast([P, tables, HD]),
@@ -376,13 +379,10 @@ def tile_gqa_flashattn_pa_t_kernel(
             )
 
         def add_turned(engine, out, ab):
-            halves = ab.rearrange("p n k (u j) -> p n k u j", u=2)
-            engine.tensor_tensor(
-                out=out.rearrange("p n (u j) -> p n u j", u=2),
-                in0=halves[:, :, 0],
-                in1=halves[:, :, 1, ::-1],
-                op=ADD,
-            )
+            for to, other in ((slice(0, HALF), slice(HALF, HD)), (slice(HALF, HD), slice(0, HALF))):
+                engine.tensor_tensor(
+                    out=out[:, :, to], in0=ab[:, :, 0, to], in1=ab[:, :, 1, other], op=ADD
+                )
 
         def finish(i, rotated, rstd):
             b, t = divmod(i, T)
@@ -407,10 +407,11 @@ def tile_gqa_flashattn_pa_t_kernel(
         waiting = []
         banks = {0: project(0, *x_mx[0])}
         neg_means = {0: means_by_scalar(banks[0])}
-        quantise_x(1, group_x(nc.vector.tensor_copy, transpose_x(1)))
+        quantise_x(1, group_x(nc.vector.tensor_copy, x_t))
         copy_ab(nc.vector.tensor_copy, 0, multiply_ab(0, psum_c, "c0"))
         add_runs(0, range(RUNS))
-        ab_1, ab_2 = multiply_ab(1, psum_c, "c1"), multiply_ab(2, psum_c, "c0")
+        ab_1 = multiply_ab(1, psum_c, "c1")
+        x_t = transpose_x(2)
         banks[1] = project(1, *x_mx[0])
         for i in range(TILES):
             b, t = divmod(i, T)
@@ -421,7 +422,7 @@ def tile_gqa_flashattn_pa_t_kernel(
                 rotated = work.tile([P, 2, NORMED, HD], F32)
             if i > 2:
                 banks[i] = project(t, *x_mx[pair])
-            gp_heads = range(GP_HEADS[0] - (pair % 3 == 0), Q_HEADS) if i in SHARED else ()
+            gp_heads = GP_HEADS if i in SHARED else ()
             rstd = measure(b, t, banks[i], neg_means[i], centred, gp_heads)
             if i == 0:
                 sums_sb = keep_sums(0)
@@ -429,12 +430,12 @@ def tile_gqa_flashattn_pa_t_kernel(
             if i == 0:
                 products(t, banks[0], neg_means[0], pair_ab, gp_heads)
                 copy_ab(nc.scalar.copy, 1, ab_1)
-                neg_means[1] = make_means(sums_sb)
+                neg_means[1] = make_means(sums_sb, psum_c, "c0")
                 add_runs(1, range(RUNS // 2))
 
             if i == 1:
                 banks[2] = project(2, *x_mx[1])
-                ab_3 = multiply_ab(3, psum_c, "c1")
+                ab_2, ab_3 = multiply_ab(2, psum_c, "c0"), multiply_ab(3, psum_c, "c1")
             if i in (2, 3):
                 c_ps.append(multiply_c(i - 2))
 
@@ -445,22 +446,25 @@ def tile_gqa_flashattn_pa_t_kernel(
             if i == 1:
                 copy_ab(nc.scalar.copy, 2, ab_2)
             if side == 1 and pair + 1 < PAIRS:
-                neg_means[i + 1] = neg_means[i + 2] = make_means(sums_sb)
+                neg_means[i + 1] = neg_means[i + 2] = make_means(sums_sb, psum_x, "x")
             if i == 1:
-                copy_ab(nc.scalar.copy, 3, ab_3)
-            if side == 0 and pair + 2 < PAIRS:
-                x_t = transpose_x(pair + 2)
-                if i > 0:
-                    x_grouped = group_x(nc.scalar.copy, x_t)
+                pass
+            if side == 0 and pair in (1, 2):
+                x_grouped = group_x(nc.scalar.copy, transpose_x(pair + 2))
+            if side == 0 and 2 <= pair < PAIRS - 3:
+                x_next = group_x(nc.scalar.copy, transpose_x(pair + 3))
             if side == 1 and pair + 2 < PAIRS:
                 add_runs(pair + 2, range(RUNS // 2))
 
             if i > 0:
-                products(t, banks[i], neg_means[i], pair_ab, gp_heads)
+                before_last = (pair + 3, x_next) if side == 1 and 2 <= pair < PAIRS - 3 else None
+                products(t, banks[i], neg_means[i], pair_ab, gp_heads, before_last)
             waiting.append((i, rotated, rstd))
+            if i == 1:
+                copy_ab(nc.vector.tensor_copy, 3, ab_3)
             if i == 0:
                 x_grouped = group_x(nc.vector.tensor_copy, x_t)
-            if side == 0 and pair + 2 < PAIRS:
+            if side == 0 and pair < 3:
                 quantise_x(pair + 2, x_grouped)
 
             single = i < 2 or TILES - 4 <= i < TILES - 1

@@ -253,25 +253,17 @@ def tile_gqa_flashattn_pa_t_kernel(
         )
         regroup_w(nc.vector.tensor_copy, wq_raw[0], 0)
         regroup_w(nc.vector.tensor_copy, wq_raw[1], W_LOAD)
-        nc.vector.tensor_tensor(
-            out=diag[:, 0:2],
-            in0=signs[:, 0:2, :].unsqueeze(2).to_broadcast([P, 2, 2, HD]),
-            in1=spread[:, 0:2, :].unsqueeze(1).to_broadcast([P, 2, 2, HD]),
-            op=MULT,
-        )
-        diagonals_for_c(spread)
         regroup_w(nc.scalar.copy, wk_raw, BANK)
         quantise_w(0, BANK)
         regroup_w(nc.vector.tensor_copy, wv_raw, BANK + W_LOAD)
-        x_grouped = group_x(nc.scalar.copy, transpose_x(0))
+        x_grouped_0 = group_x(nc.scalar.copy, transpose_x(0))
         quantise_w(BANK, BANK)
-        quantise_x(0, x_grouped)
-        x_t = transpose_x(1)
         trig_t = psum_m.tile([P, 2, T, P], BF16, tag="sums")
         for n, table in enumerate((cos_sb, sin_sb)):
             for t in range(T):
                 nc.tensor.transpose(trig_t[:, n, t, :], table[:, t, :], ident_b)
         nc.scalar.copy(out=trig[:], in_=trig_t[:])
+        x_grouped = group_x(nc.scalar.copy, transpose_x(1))
         for dst, src, per_run in ((m_codes, w_codes, RUN), (m_scales, w_scales, RUN // PACK)):
             nc.vector.tensor_copy(
                 out=dst[:].bitcast(I32).rearrange("p (i h c) -> p h i c", h=HEADS, c=per_run),
@@ -301,19 +293,6 @@ def tile_gqa_flashattn_pa_t_kernel(
         def head_of(banks, h):
             col = (h % Q_HEADS) * HD
             return banks[kind_of(h)][:, col : col + HD]
-
-        def means_by_scalar(banks):
-            neg_mean = stats.tile([P, 2, HEADS], F32)
-            unread = work.tile([P, NORMED, HD], BF16)
-            for h in ORDER:
-                nc.scalar.activation(
-                    out=unread[:, h, :],
-                    in_=head_of(banks, h),
-                    func=ACT.Copy,
-                    scale=-1.0 / HD,
-                    accum_out=neg_mean[:, 0, h : h + 1],
-                )
-            return neg_mean
 
         def measure(b, t, banks, neg_mean, centred, gp_heads):
             sum_sq = stats.tile([P, NORMED], F32)
@@ -354,11 +333,12 @@ def tile_gqa_flashattn_pa_t_kernel(
             )
             return rstd
 
-        def products(t, banks, neg_mean, pair_ab, gp_heads, before_last=None):
+        def products(t, banks, neg_mean, pair_ab, gp_heads, quantise_now):
             for h in ORDER:
                 tables = 1 if h in gp_heads else 2
-                if h == ORDER[-1] and before_last is not None:
-                    quantise_x(*before_last)
+                if h == ORDER[-1]:
+                    for pair in quantise_now:
+                        quantise_x(pair, x_grouped[pair])
                 nc.vector.scalar_tensor_tensor(
                     out=pair_ab[:, t % 2, h, 0:tables, :],
                     in0=head_of(banks, h).unsqueeze(1).to_broadcast([P, tables, HD]),
@@ -379,10 +359,13 @@ def tile_gqa_flashattn_pa_t_kernel(
             )
 
         def add_turned(engine, out, ab):
-            for to, other in ((slice(0, HALF), slice(HALF, HD)), (slice(HALF, HD), slice(0, HALF))):
-                engine.tensor_tensor(
-                    out=out[:, :, to], in0=ab[:, :, 0, to], in1=ab[:, :, 1, other], op=ADD
-                )
+            halves = ab.rearrange("p n k (u j) -> p n k u j", u=2)
+            engine.tensor_tensor(
+                out=out.rearrange("p n (u j) -> p n u j", u=2),
+                in0=halves[:, :, 0],
+                in1=halves[:, :, 1, ::-1],
+                op=ADD,
+            )
 
         def finish(i, rotated, rstd):
             b, t = divmod(i, T)
@@ -403,16 +386,31 @@ def tile_gqa_flashattn_pa_t_kernel(
                     )
             nc.sync.dma_start(out=out_1[b].rearrange("h (p t) j -> t p h j", t=T)[t], in_=k_sb[:])
 
+        quantise_x(0, x_grouped_0)
+        add_runs(0, range(RUNS))
+        nc.vector.tensor_tensor(
+            out=diag[:, 0:2],
+            in0=signs[:, 0:2, :].unsqueeze(2).to_broadcast([P, 2, 2, HD]),
+            in1=spread[:, 0:2, :].unsqueeze(1).to_broadcast([P, 2, 2, HD]),
+            op=MULT,
+        )
+        quantise_x(1, x_grouped)
+        x_grouped = {}
+        ab_0 = multiply_ab(0, psum_c, "c0")
+        banks = {0: project(0, *x_mx[0])}
+        ab_1 = multiply_ab(1, psum_c, "c1")
+        diagonals_for_c(spread)
+        copy_ab(nc.vector.tensor_copy, 0, ab_0)
+        copy_ab(nc.vector.tensor_copy, 1, ab_1)
+        sums_sb = keep_sums(0)
+        neg_means = {0: make_means(sums_sb, psum_x, "x")}
+        banks[1] = project(1, *x_mx[0])
+        add_runs(1, range(RUNS))
+        x_t = transpose_x(2)
+        ab_2, ab_3 = multiply_ab(2, psum_c, "c0"), multiply_ab(3, psum_c, "c1")
+
         c_ps = []
         waiting = []
-        banks = {0: project(0, *x_mx[0])}
-        neg_means = {0: means_by_scalar(banks[0])}
-        quantise_x(1, group_x(nc.vector.tensor_copy, x_t))
-        copy_ab(nc.vector.tensor_copy, 0, multiply_ab(0, psum_c, "c0"))
-        add_runs(0, range(RUNS))
-        ab_1 = multiply_ab(1, psum_c, "c1")
-        x_t = transpose_x(2)
-        banks[1] = project(1, *x_mx[0])
         for i in range(TILES):
             b, t = divmod(i, T)
             pair, side = divmod(i, 2)
@@ -420,55 +418,51 @@ def tile_gqa_flashattn_pa_t_kernel(
                 pair_ab = work.tile([P, 2, NORMED, 2, HD], F32)
                 centred = work.tile([P, 2, Q_HEADS, HD], F32)
                 rotated = work.tile([P, 2, NORMED, HD], F32)
-            if i > 2:
+            if i not in banks:
                 banks[i] = project(t, *x_mx[pair])
             gp_heads = GP_HEADS if i in SHARED else ()
-            rstd = measure(b, t, banks[i], neg_means[i], centred, gp_heads)
-            if i == 0:
-                sums_sb = keep_sums(0)
-
-            if i == 0:
-                products(t, banks[0], neg_means[0], pair_ab, gp_heads)
-                copy_ab(nc.scalar.copy, 1, ab_1)
-                neg_means[1] = make_means(sums_sb, psum_c, "c0")
-                add_runs(1, range(RUNS // 2))
-
-            if i == 1:
-                banks[2] = project(2, *x_mx[1])
-                ab_2, ab_3 = multiply_ab(2, psum_c, "c0"), multiply_ab(3, psum_c, "c1")
-            if i in (2, 3):
-                c_ps.append(multiply_c(i - 2))
+            rstd = measure(b, t, banks[i], neg_means[pair], centred, gp_heads)
 
             if side == 0 and pair + 1 < PAIRS:
-                add_runs(pair + 1, range(RUNS // 2, RUNS))
-            if pair + 1 < PAIRS and i in (1, *range(2, TILES, 2)):
+                if pair >= 3:
+                    add_runs(pair + 1, range(RUNS // 2, RUNS))
                 sums_sb = keep_sums(pair + 1)
-            if i == 1:
-                copy_ab(nc.scalar.copy, 2, ab_2)
             if side == 1 and pair + 1 < PAIRS:
-                neg_means[i + 1] = neg_means[i + 2] = make_means(sums_sb, psum_x, "x")
+                pool, tag = (psum_c, "c1") if i == 3 else (psum_x, "x")
+                neg_means[pair + 1] = make_means(sums_sb, pool, tag)
             if i == 1:
-                pass
-            if side == 0 and pair in (1, 2):
-                x_grouped = group_x(nc.scalar.copy, transpose_x(pair + 2))
+                banks[2] = project(2, *x_mx[1])
+                add_runs(2, range(RUNS))
+            if i == 2:
+                x_grouped[3] = group_x(nc.scalar.copy, transpose_x(3))
+            if i == 3:
+                banks[4] = project(4, *x_mx[2])
+                x_grouped[4] = group_x(nc.scalar.copy, transpose_x(4))
             if side == 0 and 2 <= pair < PAIRS - 3:
-                x_next = group_x(nc.scalar.copy, transpose_x(pair + 3))
-            if side == 1 and pair + 2 < PAIRS:
+                x_grouped[pair + 3] = group_x(nc.scalar.copy, transpose_x(pair + 3))
+            if i in (2, 3):
+                c_ps.append(multiply_c(i - 2))
+            if side == 1 and 2 <= pair < PAIRS - 2:
                 add_runs(pair + 2, range(RUNS // 2))
 
-            if i > 0:
-                before_last = (pair + 3, x_next) if side == 1 and 2 <= pair < PAIRS - 3 else None
-                products(t, banks[i], neg_means[i], pair_ab, gp_heads, before_last)
+            quantise_now = ()
+            if i == 3:
+                quantise_now = (3, 4)
+            elif side == 1 and 2 <= pair < PAIRS - 3:
+                quantise_now = (pair + 3,)
+            products(t, banks[i], neg_means[pair], pair_ab, gp_heads, quantise_now)
             waiting.append((i, rotated, rstd))
+            if i == 0:
+                x_grouped[2] = group_x(nc.vector.tensor_copy, x_t)
+                quantise_x(2, x_grouped[2])
+                copy_ab(nc.vector.tensor_copy, 2, ab_2)
             if i == 1:
                 copy_ab(nc.vector.tensor_copy, 3, ab_3)
-            if i == 0:
-                x_grouped = group_x(nc.vector.tensor_copy, x_t)
-            if side == 0 and pair < 3:
-                quantise_x(pair + 2, x_grouped)
+            if i == 3:
+                add_runs(3, range(RUNS))
 
-            single = i < 2 or TILES - 4 <= i < TILES - 1
-            if single or (side == 1 and i < TILES - 1):
+            single = TILES - 4 <= i
+            if single or side == 1:
                 mine = slice(side, side + 1) if single else slice(0, 2)
                 if gp_heads:
                     multiply_b(t if single else t - 1, mine.stop - mine.start, pair_ab, centred, gp_heads)
@@ -477,9 +471,8 @@ def tile_gqa_flashattn_pa_t_kernel(
                     rotated[:, mine].rearrange("p t h j -> p (t h) j"),
                     pair_ab[:, mine].rearrange("p t h n j -> p (t h) n j"),
                 )
-            while len(waiting) > (LAG if i < TILES - 2 else LAG - 1):
+            while len(waiting) > LAG:
                 finish(*waiting[0])
                 waiting = waiting[1:]
-        add_turned(nc.vector, rotated[:, 1], pair_ab[:, 1])
         for tile in waiting:
             finish(*tile)

@@ -29,7 +29,7 @@ HEADS = Q_HEADS + 2 * KV_HEADS
 RUNS = HD // RUN
 GP_HEADS = range(3, Q_HEADS)
 TILES = B * T
-SHARED = range(4, TILES - 1)
+SHARED = range(4, TILES - 2)
 LAG = 3
 PAIRS = TILES // 2
 W_LOAD = 256
@@ -120,9 +120,9 @@ def tile_gqa_flashattn_pa_t_kernel(
         def regroup_w(copy, raw, first_col):
             copy(
                 out=w_grouped[:, first_col * PACK : (first_col + W_LOAD) * PACK].rearrange(
-                    "p (c v) -> p c v", v=PACK
+                    "p (c i v) -> p c v i", i=4, v=PACK
                 ),
-                in_=raw[:].rearrange("p v c -> p c v"),
+                in_=raw[:].rearrange("p v (c i) -> p c v i", i=4),
             )
 
         def quantise_w(first_col, cols):
@@ -333,9 +333,9 @@ def tile_gqa_flashattn_pa_t_kernel(
             )
             return rstd
 
-        def products(t, banks, neg_mean, pair_ab, gp_heads, quantise_now):
-            for h in ORDER:
-                tables = 1 if h in gp_heads else 2
+        def products(t, banks, neg_mean, pair_ab, gp_heads, gp_tables, quantise_now):
+            shares = [(h, 2 - gp_tables if h in gp_heads else 2) for h in ORDER]
+            for h, tables in [share for share in shares if share[1] > 0]:
                 if h == ORDER[-1]:
                     for pair in quantise_now:
                         quantise_x(pair, x_grouped[pair])
@@ -348,15 +348,16 @@ def tile_gqa_flashattn_pa_t_kernel(
                     op1=MULT,
                 )
 
-        def multiply_b(t0, count, pair_ab, centred, gp_heads):
+        def multiply_gp(t0, count, pair_ab, centred, gp_heads, gp_tables):
             mine = slice(t0 % 2, t0 % 2 + count)
-            heads = len(gp_heads)
-            nc.gpsimd.tensor_tensor(
-                out=pair_ab[:, mine, gp_heads[0] : Q_HEADS, 1, :],
-                in0=centred[:, mine, gp_heads[0] : Q_HEADS],
-                in1=tab_ab[:, t0 : t0 + count, 1, 0:1, :].to_broadcast([P, count, heads, HD]),
-                op=MULT,
-            )
+            first = 2 - gp_tables
+            for h in gp_heads:
+                nc.gpsimd.tensor_tensor(
+                    out=pair_ab[:, mine, h, first:2],
+                    in0=centred[:, mine, h].unsqueeze(2).to_broadcast([P, count, gp_tables, HD]),
+                    in1=tab_ab[:, t0 : t0 + count, first:2, 0, :],
+                    op=MULT,
+                )
 
         def add_turned(engine, out, ab):
             halves = ab.rearrange("p n k (u j) -> p n k u j", u=2)
@@ -396,18 +397,17 @@ def tile_gqa_flashattn_pa_t_kernel(
         )
         quantise_x(1, x_grouped)
         x_grouped = {}
-        ab_0 = multiply_ab(0, psum_c, "c0")
         banks = {0: project(0, *x_mx[0])}
-        ab_1 = multiply_ab(1, psum_c, "c1")
+        ab_0 = multiply_ab(0, psum_c, "c0")
         diagonals_for_c(spread)
         copy_ab(nc.vector.tensor_copy, 0, ab_0)
+        neg_means = {0: make_means(keep_sums(0), psum_x, "x")}
+        ab_1 = multiply_ab(1, psum_c, "c1")
         copy_ab(nc.vector.tensor_copy, 1, ab_1)
-        sums_sb = keep_sums(0)
-        neg_means = {0: make_means(sums_sb, psum_x, "x")}
         banks[1] = project(1, *x_mx[0])
         add_runs(1, range(RUNS))
         x_t = transpose_x(2)
-        ab_2, ab_3 = multiply_ab(2, psum_c, "c0"), multiply_ab(3, psum_c, "c1")
+        ab_2 = multiply_ab(2, psum_c, "c0")
 
         c_ps = []
         waiting = []
@@ -428,10 +428,11 @@ def tile_gqa_flashattn_pa_t_kernel(
                     add_runs(pair + 1, range(RUNS // 2, RUNS))
                 sums_sb = keep_sums(pair + 1)
             if side == 1 and pair + 1 < PAIRS:
-                pool, tag = (psum_c, "c1") if i == 3 else (psum_x, "x")
+                pool, tag = (psum_c, "c1") if i < 4 else (psum_x, "x")
                 neg_means[pair + 1] = make_means(sums_sb, pool, tag)
             if i == 1:
                 banks[2] = project(2, *x_mx[1])
+                ab_3 = multiply_ab(3, psum_c, "c1")
                 add_runs(2, range(RUNS))
             if i == 2:
                 x_grouped[3] = group_x(nc.scalar.copy, transpose_x(3))
@@ -450,7 +451,8 @@ def tile_gqa_flashattn_pa_t_kernel(
                 quantise_now = (3, 4)
             elif side == 1 and 2 <= pair < PAIRS - 3:
                 quantise_now = (pair + 3,)
-            products(t, banks[i], neg_means[pair], pair_ab, gp_heads, quantise_now)
+            gp_tables = 1 if pair < PAIRS - 3 else 2
+            products(t, banks[i], neg_means[pair], pair_ab, gp_heads, gp_tables, quantise_now)
             waiting.append((i, rotated, rstd))
             if i == 0:
                 x_grouped[2] = group_x(nc.vector.tensor_copy, x_t)
@@ -465,7 +467,9 @@ def tile_gqa_flashattn_pa_t_kernel(
             if single or side == 1:
                 mine = slice(side, side + 1) if single else slice(0, 2)
                 if gp_heads:
-                    multiply_b(t if single else t - 1, mine.stop - mine.start, pair_ab, centred, gp_heads)
+                    multiply_gp(
+                        t if single else t - 1, mine.stop - mine.start, pair_ab, centred, gp_heads, gp_tables
+                    )
                 add_turned(
                     nc.gpsimd,
                     rotated[:, mine].rearrange("p t h j -> p (t h) j"),

@@ -335,8 +335,9 @@ def tile_gqa_flashattn_pa_t_kernel(
 
         def products(t, banks, neg_mean, pair_ab, gp_heads, gp_tables, quantise_now):
             shares = [(h, 2 - gp_tables if h in gp_heads else 2) for h in ORDER]
-            for h, tables in [share for share in shares if share[1] > 0]:
-                if h == ORDER[-1]:
+            mine = [share for share in shares if share[1] > 0]
+            for h, tables in mine:
+                if h == mine[-1][0]:
                     for pair in quantise_now:
                         quantise_x(pair, x_grouped[pair])
                 nc.vector.scalar_tensor_tensor(
@@ -451,7 +452,7 @@ def tile_gqa_flashattn_pa_t_kernel(
                 quantise_now = (3, 4)
             elif side == 1 and 2 <= pair < PAIRS - 3:
                 quantise_now = (pair + 3,)
-            gp_tables = 1 if pair < PAIRS - 3 else 2
+            gp_tables = 2
             products(t, banks[i], neg_means[pair], pair_ab, gp_heads, gp_tables, quantise_now)
             waiting.append((i, rotated, rstd))
             if i == 0:

@@ -333,11 +333,11 @@ def tile_gqa_flashattn_pa_t_kernel(
             )
             return rstd
 
-        def products(t, banks, neg_mean, pair_ab, gp_heads, gp_tables, quantise_now):
+        def products(b, t, banks, neg_mean, pair_ab, gp_heads, gp_tables, quantise_now):
             shares = [(h, 2 - gp_tables if h in gp_heads else 2) for h in ORDER]
             mine = [share for share in shares if share[1] > 0]
             for h, tables in mine:
-                if h == mine[-1][0]:
+                if h == mine[1 if b * T + t >= 4 else -1][0]:
                     for pair in quantise_now:
                         quantise_x(pair, x_grouped[pair])
                 nc.vector.scalar_tensor_tensor(
@@ -453,7 +453,7 @@ def tile_gqa_flashattn_pa_t_kernel(
             elif side == 1 and 2 <= pair < PAIRS - 3:
                 quantise_now = (pair + 3,)
             gp_tables = 2
-            products(t, banks[i], neg_means[pair], pair_ab, gp_heads, gp_tables, quantise_now)
+            products(b, t, banks[i], neg_means[pair], pair_ab, gp_heads, gp_tables, quantise_now)
             waiting.append((i, rotated, rstd))
             if i == 0:
                 x_grouped[2] = group_x(nc.vector.tensor_copy, x_t)

@@ -65,10 +65,9 @@ def tile_gqa_flashattn_pa_t_kernel(
         warm = const.tile([P, 1], F32)
         nc.scalar.activation(out=warm[:], in_=eps[:], func=ACT.Abs_reciprocal_sqrt)
 
-        def load_w(w, name, first_col=0):
-            raw = const.tile([P, PACK, W_LOAD], BF16, name=name)
-            rows = w.rearrange("(p v) c -> p v c", v=PACK)
-            nc.sync.dma_start(out=raw[:], in_=rows[:, :, first_col : first_col + W_LOAD])
+        def load_w(w, name):
+            raw = const.tile([P, PACK, w.shape[1]], BF16, name=name)
+            nc.sync.dma_start(out=raw[:], in_=w.rearrange("(p v) c -> p v c", v=PACK))
             return raw
 
         def load_x(b, pair):
@@ -78,15 +77,14 @@ def tile_gqa_flashattn_pa_t_kernel(
             )
             return x_sb
 
-        wq_raw = [load_w(Wq, "wq_raw0")]
+        wq_raw = load_w(Wq, "wq_raw")
+        x_pairs = [load_x(0, 0)]
+        wk_raw = load_w(Wk, "wk_raw")
+        wv_raw = load_w(Wv, "wv_raw")
         for n, vec in enumerate((q_gamma, k_gamma, q_beta, k_beta)):
             nc.sync.dma_start(
                 out=vecs[0:1, n * HD : (n + 1) * HD], in_=vec.rearrange("(o j) -> o j", o=1)
             )
-        wq_raw.append(load_w(Wq, "wq_raw1", W_LOAD))
-        wk_raw = load_w(Wk, "wk_raw")
-        wv_raw = load_w(Wv, "wv_raw")
-        x_pairs = [load_x(0, 0)]
         cos_sb = const.tile([P, T, HD], BF16)
         nc.sync.dma_start(out=cos_sb[:], in_=cos.rearrange("(p t) j -> p t j", t=T))
         sin_sb = const.tile([P, T, HD], BF16)
@@ -117,12 +115,12 @@ def tile_gqa_flashattn_pa_t_kernel(
         m_codes = const.tile([P, W_COLS], U32, align_bytes=64)
         m_scales = const.tile([P, W_COLS], U8, align_bytes=64)
 
-        def regroup_w(copy, raw, first_col):
+        def regroup_w(copy, raw, first_col, raw_col=0):
             copy(
                 out=w_grouped[:, first_col * PACK : (first_col + W_LOAD) * PACK].rearrange(
                     "p (c i v) -> p c v i", i=4, v=PACK
                 ),
-                in_=raw[:].rearrange("p v (c i) -> p c v i", i=4),
+                in_=raw[:, :, raw_col : raw_col + W_LOAD].rearrange("p v (c i) -> p c v i", i=4),
             )
 
         def quantise_w(first_col, cols):
@@ -201,36 +199,55 @@ def tile_gqa_flashattn_pa_t_kernel(
         trig = const.tile([P, 2, T, P], BF16)
         tab_ab = const.tile([P, T, 2, 2, HD], F32)
 
-        def multiply_ab(t, pool, tag):
-            ab = pool.tile([P, 2, 2 * HD], F32, tag=tag, name="ab")
-            for n in range(2):
-                nc.tensor.matmul(
-                    out=ab[:, n, :],
-                    lhsT=trig[:, n, t, :],
-                    rhs=diag[:, n].rearrange("p k j -> p (k j)"),
-                    start=True,
-                    stop=True,
-                )
-            return ab
-
-        def copy_ab(copy, t, ab):
-            copy(
-                out=tab_ab[:, t].rearrange("p n k j -> p (n k j)"),
-                in_=ab[:].rearrange("p n c -> p (n c)"),
+        def first_ab(spread):
+            nc.vector.tensor_tensor(
+                out=tab_ab[:, 0, 0],
+                in0=spread[:, 0:2, :],
+                in1=cos_sb[:, 0:1].to_broadcast([P, 2, HD]),
+                op=MULT,
+            )
+            nc.vector.tensor_tensor(
+                out=tab_ab[:, 0, 1, :, 0:HALF],
+                in0=spread[:, 0:2, 0:HALF],
+                in1=sin_sb[:, 0:1, HALF:HD].to_broadcast([P, 2, HALF]),
+                op=MULT,
+            )
+            nc.vector.scalar_tensor_tensor(
+                out=tab_ab[:, 0, 1, :, HALF:HD],
+                in0=spread[:, 0:2, HALF:HD],
+                scalar=-1.0,
+                in1=sin_sb[:, 0:1, 0:HALF].to_broadcast([P, 2, HALF]),
+                op0=MULT,
+                op1=MULT,
             )
 
-        def diagonals_for_c(spread):
-            nc.vector.tensor_tensor(
+        def make_ab(t):
+            nc.gpsimd.tensor_tensor(
+                out=tab_ab[:, t, 0],
+                in0=gammas[:, 0:2, :],
+                in1=cos_sb[:, t : t + 1].to_broadcast([P, 2, HD]),
+                op=MULT,
+            )
+            sin_halves = sin_sb[:, t : t + 1].rearrange("p k (u j) -> p k u j", u=2)
+            nc.gpsimd.tensor_tensor(
+                out=tab_ab[:, t, 1].rearrange("p k (u j) -> p k u j", u=2),
+                in0=signed[:].rearrange("p k (u j) -> p k u j", u=2),
+                in1=sin_halves[:, :, ::-1].to_broadcast([P, 2, 2, HALF]),
+                op=MULT,
+            )
+
+        def diagonals_for_c():
+            nc.gpsimd.tensor_tensor(
                 out=diag[:, 2],
                 in0=signs[:, 0:1, :].to_broadcast([P, 2, HD]),
-                in1=spread[:, 2:4, :],
+                in1=gammas[:, 2:4, :],
                 op=MULT,
             )
             for to, other in ((slice(0, HALF), slice(HALF, HD)), (slice(HALF, HD), slice(0, HALF))):
-                nc.vector.tensor_tensor(
+                nc.gpsimd.tensor_tensor(
                     out=diag[:, 3, :, to],
                     in0=signs[:, 2:3, to].to_broadcast([P, 2, HALF]),
-                    in1=spread[:, 2:4, other],
+                    in1=gammas[:, 2:4, other],
                     op=MULT,
                 )
 
@@ -247,28 +264,24 @@ def tile_gqa_flashattn_pa_t_kernel(
                     )
             return c_bank
 
-        spread = psum_u.tile([P, 4, HD], F32, tag="u_kv")
+        gammas = const.tile([P, 4, HD], F32)
+        signed = const.tile([P, 2, HD], F32)
+        regroup_w(nc.vector.tensor_copy, wq_raw, 0)
+        regroup_w(nc.vector.tensor_copy, wq_raw, W_LOAD, W_LOAD)
+        regroup_w(nc.scalar.copy, wk_raw, BANK)
+        quantise_w(0, BANK)
+        x_grouped_0 = group_x(nc.scalar.copy, transpose_x(0))
+        spread = psum_c.tile([P, 4, HD], F32, tag="c1")
         nc.tensor.matmul(
             out=spread[:].rearrange("p n j -> p (n j)"), lhsT=ones[:], rhs=vecs[:], start=True, stop=True
         )
-        regroup_w(nc.vector.tensor_copy, wq_raw[0], 0)
-        regroup_w(nc.vector.tensor_copy, wq_raw[1], W_LOAD)
-        regroup_w(nc.scalar.copy, wk_raw, BANK)
-        quantise_w(0, BANK)
+        nc.scalar.copy(out=gammas[:], in_=spread[:])
+        nc.scalar.copy(out=signed[:, :, 0:HALF], in_=spread[:, 0:2, 0:HALF])
+        nc.scalar.activation(
+            out=signed[:, :, HALF:HD], in_=spread[:, 0:2, HALF:HD], func=ACT.Copy, scale=-1.0
+        )
         regroup_w(nc.vector.tensor_copy, wv_raw, BANK + W_LOAD)
-        x_grouped_0 = group_x(nc.scalar.copy, transpose_x(0))
         quantise_w(BANK, BANK)
-        trig_t = psum_m.tile([P, 2, T, P], BF16, tag="sums")
-        for n, table in enumerate((cos_sb, sin_sb)):
-            for t in range(T):
-                nc.tensor.transpose(trig_t[:, n, t, :], table[:, t, :], ident_b)
-        nc.scalar.copy(out=trig[:], in_=trig_t[:])
-        x_grouped = group_x(nc.scalar.copy, transpose_x(1))
-        for dst, src, per_run in ((m_codes, w_codes, RUN), (m_scales, w_scales, RUN // PACK)):
-            nc.vector.tensor_copy(
-                out=dst[:].bitcast(I32).rearrange("p (i h c) -> p h i c", h=HEADS, c=per_run),
-                in_=src[:].bitcast(I32).rearrange("p (h i c) -> p h i c", h=HEADS, c=per_run),
-            )
 
         def kind_of(h):
             return 0 if h < Q_HEADS else 1
@@ -294,7 +307,7 @@ def tile_gqa_flashattn_pa_t_kernel(
             col = (h % Q_HEADS) * HD
             return banks[kind_of(h)][:, col : col + HD]
 
-        def measure(b, t, banks, neg_mean, centred, gp_heads):
+        def measure(b, t, banks, neg_mean, centred, gp_heads, between=None):
             sum_sq = stats.tile([P, NORMED], F32)
             unread = work.tile([P, NORMED, HD], BF16)
             for h in ORDER:
@@ -315,6 +328,8 @@ def tile_gqa_flashattn_pa_t_kernel(
                     nc.sync.dma_start(
                         out=out_2[b].rearrange("h (p t) j -> t p h j", t=T)[t], in_=v_sb[:]
                     )
+                    if between:
+                        between()
             for h in gp_heads:
                 nc.scalar.activation(
                     out=centred[:, t % 2, h, :],
@@ -337,6 +352,8 @@ def tile_gqa_flashattn_pa_t_kernel(
             shares = [(h, 2 - gp_tables if h in gp_heads else 2) for h in ORDER]
             mine = [share for share in shares if share[1] > 0]
             for h, tables in mine:
+                if b * T + t == 2 and h == mine[-1][0]:
+                    x_grouped[3] = group_x(nc.vector.tensor_copy, x_t)
                 if h == mine[1 if b * T + t >= 4 else -1][0]:
                     for pair in quantise_now:
                         quantise_x(pair, x_grouped[pair])
@@ -389,27 +406,38 @@ def tile_gqa_flashattn_pa_t_kernel(
             nc.sync.dma_start(out=out_1[b].rearrange("h (p t) j -> t p h j", t=T)[t], in_=k_sb[:])
 
         quantise_x(0, x_grouped_0)
+        banks = {0: project(0, *x_mx[0])}
+        x_t = transpose_x(1)
+        trig_t = psum_c.tile([P, 2, T, P], BF16, tag="c0")
+        for n, table in enumerate((cos_sb, sin_sb)):
+            for t in range(T):
+                nc.tensor.transpose(trig_t[:, n, t, :], table[:, t, :], ident_b)
+        x_grouped = group_x(nc.scalar.copy, x_t)
+        nc.scalar.copy(out=trig[:], in_=trig_t[:])
+        for dst, src, per_run in ((m_codes, w_codes, RUN), (m_scales, w_scales, RUN // PACK)):
+            nc.vector.tensor_copy(
+                out=dst[:].bitcast(I32).rearrange("p (i h c) -> p h i c", h=HEADS, c=per_run),
+                in_=src[:].bitcast(I32).rearrange("p (h i c) -> p h i c", h=HEADS, c=per_run),
+            )
         add_runs(0, range(RUNS))
-        nc.vector.tensor_tensor(
-            out=diag[:, 0:2],
-            in0=signs[:, 0:2, :].unsqueeze(2).to_broadcast([P, 2, 2, HD]),
-            in1=spread[:, 0:2, :].unsqueeze(1).to_broadcast([P, 2, 2, HD]),
-            op=MULT,
-        )
+        first_sums = const.tile([P, NORMED], F32)
+        first_means = const.tile([P, 2, NORMED], F32)
+        for part, (heads, bank) in enumerate(((range(0, Q_HEADS), banks[0][0]), (range(Q_HEADS, NORMED), banks[0][1]))):
+            nc.vector.tensor_reduce(
+                out=first_sums[:, heads.start : heads.stop],
+                in_=bank[:, 0 : len(heads) * HD].rearrange("p (h j) -> p h j", j=HD),
+                axis=mybir.AxisListType.X,
+                op=ADD,
+            )
+        nc.scalar.activation(out=first_means[:, 0, :], in_=first_sums[:], func=ACT.Copy, scale=-1.0 / HD)
+        first_ab(spread)
         quantise_x(1, x_grouped)
         x_grouped = {}
-        banks = {0: project(0, *x_mx[0])}
-        ab_0 = multiply_ab(0, psum_c, "c0")
-        diagonals_for_c(spread)
-        copy_ab(nc.vector.tensor_copy, 0, ab_0)
-        neg_means = {0: make_means(keep_sums(0), psum_x, "x")}
-        ab_1 = multiply_ab(1, psum_c, "c1")
-        copy_ab(nc.vector.tensor_copy, 1, ab_1)
+        for t in range(1, T):
+            make_ab(t)
+        diagonals_for_c()
+        neg_means = {}
         banks[1] = project(1, *x_mx[0])
-        add_runs(1, range(RUNS))
-        x_t = transpose_x(2)
-        ab_2 = multiply_ab(2, psum_c, "c0")
-
         c_ps = []
         waiting = []
         for i in range(TILES):
@@ -422,24 +450,32 @@ def tile_gqa_flashattn_pa_t_kernel(
             if i not in banks:
                 banks[i] = project(t, *x_mx[pair])
             gp_heads = GP_HEADS if i in SHARED else ()
-            rstd = measure(b, t, banks[i], neg_means[pair], centred, gp_heads)
+            neg_mean = neg_means[pair] if i > 0 else first_means
+            kept = []
+            rstd = measure(b, t, banks[i], neg_mean, centred, gp_heads, (lambda: kept.append(keep_sums(i))) if i < 2 else None)
+            if i < 2:
+                neg_means[i] = make_means(kept[0], psum_c, "c0")
+            if i == 0:
+                add_runs(1, range(RUNS))
+                x_t = transpose_x(2)
 
-            if side == 0 and pair + 1 < PAIRS:
+            if side == 0 and 0 < pair < PAIRS - 1:
                 if pair >= 3:
                     add_runs(pair + 1, range(RUNS // 2, RUNS))
                 sums_sb = keep_sums(pair + 1)
-            if side == 1 and pair + 1 < PAIRS:
+            if side == 1 and 0 < pair < PAIRS - 1:
                 pool, tag = (psum_c, "c1") if i < 4 else (psum_x, "x")
                 neg_means[pair + 1] = make_means(sums_sb, pool, tag)
             if i == 1:
                 banks[2] = project(2, *x_mx[1])
-                ab_3 = multiply_ab(3, psum_c, "c1")
                 add_runs(2, range(RUNS))
             if i == 2:
-                x_grouped[3] = group_x(nc.scalar.copy, transpose_x(3))
+                banks[3] = project(3, *x_mx[1])
+                x_t = transpose_x(3)
             if i == 3:
                 banks[4] = project(4, *x_mx[2])
-                x_grouped[4] = group_x(nc.scalar.copy, transpose_x(4))
+                x_t = transpose_x(4)
+                x_grouped[4] = group_x(nc.scalar.copy, x_t)
             if side == 0 and 2 <= pair < PAIRS - 3:
                 x_grouped[pair + 3] = group_x(nc.scalar.copy, transpose_x(pair + 3))
             if i in (2, 3):
@@ -453,14 +489,11 @@ def tile_gqa_flashattn_pa_t_kernel(
             elif side == 1 and 2 <= pair < PAIRS - 3:
                 quantise_now = (pair + 3,)
             gp_tables = 2
-            products(b, t, banks[i], neg_means[pair], pair_ab, gp_heads, gp_tables, quantise_now)
+            products(b, t, banks[i], neg_mean, pair_ab, gp_heads, gp_tables, quantise_now)
             waiting.append((i, rotated, rstd))
             if i == 0:
                 x_grouped[2] = group_x(nc.vector.tensor_copy, x_t)
                 quantise_x(2, x_grouped[2])
-                copy_ab(nc.vector.tensor_copy, 2, ab_2)
-            if i == 1:
-                copy_ab(nc.vector.tensor_copy, 3, ab_3)
             if i == 3:
                 add_runs(3, range(RUNS))
 

@@ -30,6 +30,7 @@ RUNS = HD // RUN
 GP_HEADS = range(3, Q_HEADS)
 TILES = B * T
 SHARED = range(4, TILES - 2)
+LAST_SHARED = range(TILES - 4, TILES - 2)
 LAG = 3
 PAIRS = TILES // 2
 W_LOAD = 256
@@ -488,7 +489,7 @@ def tile_gqa_flashattn_pa_t_kernel(
                 quantise_now = (3, 4)
             elif side == 1 and 2 <= pair < PAIRS - 3:
                 quantise_now = (pair + 3,)
-            gp_tables = 2
+            gp_tables = 1 if i in LAST_SHARED else 2
             products(b, t, banks[i], neg_mean, pair_ab, gp_heads, gp_tables, quantise_now)
             waiting.append((i, rotated, rstd))
             if i == 0:

@@ -353,6 +353,9 @@ def tile_gqa_flashattn_pa_t_kernel(
             shares = [(h, 2 - gp_tables if h in gp_heads else 2) for h in ORDER]
             mine = [share for share in shares if share[1] > 0]
             for h, tables in mine:
+                if b * T + t == 1 and h == 0:
+                    x_grouped[2] = group_x(nc.vector.tensor_copy, x_t)
+                    quantise_x(2, x_grouped[2])
                 if b * T + t == 2 and h == mine[-1][0]:
                     x_grouped[3] = group_x(nc.vector.tensor_copy, x_t)
                 if h == mine[1 if b * T + t >= 4 else -1][0]:
@@ -414,7 +417,6 @@ def tile_gqa_flashattn_pa_t_kernel(
             for t in range(T):
                 nc.tensor.transpose(trig_t[:, n, t, :], table[:, t, :], ident_b)
         x_grouped = group_x(nc.scalar.copy, x_t)
-        nc.scalar.copy(out=trig[:], in_=trig_t[:])
         for dst, src, per_run in ((m_codes, w_codes, RUN), (m_scales, w_scales, RUN // PACK)):
             nc.vector.tensor_copy(
                 out=dst[:].bitcast(I32).rearrange("p (i h c) -> p h i c", h=HEADS, c=per_run),
@@ -432,11 +434,12 @@ def tile_gqa_flashattn_pa_t_kernel(
             )
         nc.scalar.activation(out=first_means[:, 0, :], in_=first_sums[:], func=ACT.Copy, scale=-1.0 / HD)
         first_ab(spread)
+        nc.vector.tensor_copy(out=trig[:], in_=trig_t[:])
         quantise_x(1, x_grouped)
         x_grouped = {}
+        diagonals_for_c()
         for t in range(1, T):
             make_ab(t)
-        diagonals_for_c()
         neg_means = {}
         banks[1] = project(1, *x_mx[0])
         c_ps = []
@@ -460,44 +463,33 @@ def tile_gqa_flashattn_pa_t_kernel(
                 add_runs(1, range(RUNS))
                 x_t = transpose_x(2)
 
+            if side == 0 and 2 <= pair < PAIRS - 2:
+                x_grouped[pair + 2] = group_x(nc.scalar.copy, transpose_x(pair + 2))
             if side == 0 and 0 < pair < PAIRS - 1:
-                if pair >= 3:
-                    add_runs(pair + 1, range(RUNS // 2, RUNS))
+                if pair >= 2:
+                    add_runs(pair + 1, range(RUNS))
                 sums_sb = keep_sums(pair + 1)
             if side == 1 and 0 < pair < PAIRS - 1:
                 pool, tag = (psum_c, "c1") if i < 4 else (psum_x, "x")
                 neg_means[pair + 1] = make_means(sums_sb, pool, tag)
             if i == 1:
                 banks[2] = project(2, *x_mx[1])
-                add_runs(2, range(RUNS))
             if i == 2:
                 banks[3] = project(3, *x_mx[1])
                 x_t = transpose_x(3)
             if i == 3:
                 banks[4] = project(4, *x_mx[2])
-                x_t = transpose_x(4)
-                x_grouped[4] = group_x(nc.scalar.copy, x_t)
-            if side == 0 and 2 <= pair < PAIRS - 3:
-                x_grouped[pair + 3] = group_x(nc.scalar.copy, transpose_x(pair + 3))
             if i in (2, 3):
                 c_ps.append(multiply_c(i - 2))
-            if side == 1 and 2 <= pair < PAIRS - 2:
-                add_runs(pair + 2, range(RUNS // 2))
 
             quantise_now = ()
-            if i == 3:
-                quantise_now = (3, 4)
-            elif side == 1 and 2 <= pair < PAIRS - 3:
-                quantise_now = (pair + 3,)
+            if side == 1 and 1 <= pair < PAIRS - 2:
+                quantise_now = (pair + 2,)
             gp_tables = 1 if i in LAST_SHARED else 2
             products(b, t, banks[i], neg_mean, pair_ab, gp_heads, gp_tables, quantise_now)
             waiting.append((i, rotated, rstd))
-            if i == 0:
-                x_grouped[2] = group_x(nc.vector.tensor_copy, x_t)
-                quantise_x(2, x_grouped[2])
-            if i == 3:
-                add_runs(3, range(RUNS))
-
+            if i == 1:
+                add_runs(2, range(RUNS))
             single = TILES - 4 <= i
             if single or side == 1:
                 mine = slice(side, side + 1) if single else slice(0, 2)

@@ -30,7 +30,6 @@ RUNS = HD // RUN
 GP_HEADS = range(3, Q_HEADS)
 TILES = B * T
 SHARED = range(4, TILES - 2)
-LAST_SHARED = range(TILES - 4, TILES - 2)
 LAG = 3
 PAIRS = TILES // 2
 W_LOAD = 256
@@ -485,23 +484,24 @@ def tile_gqa_flashattn_pa_t_kernel(
             quantise_now = ()
             if side == 1 and 1 <= pair < PAIRS - 2:
                 quantise_now = (pair + 2,)
-            gp_tables = 1 if i in LAST_SHARED else 2
+            gp_tables = 2
             products(b, t, banks[i], neg_mean, pair_ab, gp_heads, gp_tables, quantise_now)
             waiting.append((i, rotated, rstd))
             if i == 1:
                 add_runs(2, range(RUNS))
-            single = TILES - 4 <= i
+            single = TILES - 2 <= i
             if single or side == 1:
                 mine = slice(side, side + 1) if single else slice(0, 2)
                 if gp_heads:
                     multiply_gp(
                         t if single else t - 1, mine.stop - mine.start, pair_ab, centred, gp_heads, gp_tables
                     )
-                add_turned(
-                    nc.gpsimd,
-                    rotated[:, mine].rearrange("p t h j -> p (t h) j"),
-                    pair_ab[:, mine].rearrange("p t h n j -> p (t h) n j"),
-                )
+                for heads in (slice(0, 4), slice(4, 6)) if i == TILES - 1 else (slice(0, NORMED),):
+                    add_turned(
+                        nc.gpsimd,
+                        rotated[:, mine, heads].rearrange("p t h j -> p (t h) j"),
+                        pair_ab[:, mine, heads].rearrange("p t h n j -> p (t h) n j"),
+                    )
             while len(waiting) > LAG:
                 finish(*waiting[0])
                 waiting = waiting[1:]

@@ -466,7 +466,7 @@ def tile_gqa_flashattn_pa_t_kernel(
                 x_grouped[pair + 2] = group_x(nc.scalar.copy, transpose_x(pair + 2))
             if side == 0 and 0 < pair < PAIRS - 1:
                 if pair >= 2:
-                    add_runs(pair + 1, range(RUNS))
+                    add_runs(pair + 1, range(RUNS // 2 if pair > 2 else 0, RUNS))
                 sums_sb = keep_sums(pair + 1)
             if side == 1 and 0 < pair < PAIRS - 1:
                 pool, tag = (psum_c, "c1") if i < 4 else (psum_x, "x")
@@ -489,6 +489,9 @@ def tile_gqa_flashattn_pa_t_kernel(
             waiting.append((i, rotated, rstd))
             if i == 1:
                 add_runs(2, range(RUNS))
+            if side == 1 and 2 <= pair < PAIRS - 2:
+                banks[i + 1] = project((t + 1) % T, *x_mx[pair + 1])
+                add_runs(pair + 2, range(RUNS // 2))
             single = TILES - 2 <= i
             if single or side == 1:
                 mine = slice(side, side + 1) if single else slice(0, 2)

@@ -462,15 +462,17 @@ def tile_gqa_flashattn_pa_t_kernel(
                 add_runs(1, range(RUNS))
                 x_t = transpose_x(2)
 
-            if side == 0 and 2 <= pair < PAIRS - 2:
-                x_grouped[pair + 2] = group_x(nc.scalar.copy, transpose_x(pair + 2))
+            if i == 4:
+                x_grouped[4] = group_x(nc.scalar.copy, transpose_x(4))
             if side == 0 and 0 < pair < PAIRS - 1:
                 if pair >= 2:
                     add_runs(pair + 1, range(RUNS // 2 if pair > 2 else 0, RUNS))
                 sums_sb = keep_sums(pair + 1)
             if side == 1 and 0 < pair < PAIRS - 1:
-                pool, tag = (psum_c, "c1") if i < 4 else (psum_x, "x")
+                pool, tag = (psum_c, "c1") if i < 4 else (psum_m, "sums")
                 neg_means[pair + 1] = make_means(sums_sb, pool, tag)
+            if side == 1 and 2 <= pair < PAIRS - 3:
+                x_grouped[pair + 3] = group_x(nc.scalar.copy, transpose_x(pair + 3))
             if i == 1:
                 banks[2] = project(2, *x_mx[1])
             if i == 2:

@@ -311,6 +311,15 @@ def tile_gqa_flashattn_pa_t_kernel(
             sum_sq = stats.tile([P, NORMED], F32)
             unread = work.tile([P, NORMED, HD], BF16)
             for h in ORDER:
+                if h == 0:
+                    for gp_head in gp_heads:
+                        nc.scalar.activation(
+                            out=centred[:, t % 2, gp_head, :],
+                            in_=head_of(banks, gp_head),
+                            func=ACT.Identity,
+                            bias=neg_mean[:, t % 2, gp_head : gp_head + 1],
+                            scale=1.0,
+                        )
                 nc.scalar.activation(
                     out=unread[:, h, :],
                     in_=head_of(banks, h),
@@ -330,14 +339,6 @@ def tile_gqa_flashattn_pa_t_kernel(
                     )
                     if between:
                         between()
-            for h in gp_heads:
-                nc.scalar.activation(
-                    out=centred[:, t % 2, h, :],
-                    in_=head_of(banks, h),
-                    func=ACT.Identity,
-                    bias=neg_mean[:, t % 2, h : h + 1],
-                    scale=1.0,
-                )
             rstd = stats.tile([P, NORMED], F32)
             nc.scalar.activation(
                 out=rstd[:],

from contextlib import ExitStack

import concourse.mybir as mybir
from concourse.masks import make_identity

F32 = mybir.dt.float32
BF16 = mybir.dt.bfloat16
U32 = mybir.dt.uint32
U8 = mybir.dt.uint8
I32 = mybir.dt.int32
FP8X4 = mybir.dt.float8_e4m3fn_x4
ADD = mybir.AluOpType.add
MULT = mybir.AluOpType.mult
ACT = mybir.ActivationFunctionType

P = 128
PACK = 4
RUN = 16
B, S, D = 8, 512, 512
HD = 128
HALF = HD // 2
Q_HEADS, KV_HEADS = 4, 2
NORMED = Q_HEADS + KV_HEADS
T = S // P
BANK = 512
W_COLS = (Q_HEADS + 2 * KV_HEADS) * HD
EPS = 1e-6
HEADS = Q_HEADS + 2 * KV_HEADS
RUNS = HD // RUN
GP_HEADS = range(3, Q_HEADS)
TILES = B * T
SHARED = range(4, TILES - 2)
LAG = 3
PAIRS = TILES // 2
W_LOAD = 256
ORDER = (*range(Q_HEADS, NORMED), *range(Q_HEADS))

FLOPS = 2 * B * S * D * W_COLS


def tile_gqa_flashattn_pa_t_kernel(
    tc, x, cos, sin, Wq, Wk, Wv, q_gamma, q_beta, k_gamma, k_beta, out_0, out_1, out_2
):
    nc = tc.nc
    with ExitStack() as ctx:
        const = ctx.enter_context(tc.tile_pool(name="const", bufs=1))
        xprep = ctx.enter_context(tc.tile_pool(name="xprep", bufs=6))
        stats = ctx.enter_context(tc.tile_pool(name="stats", bufs=8))
        work = ctx.enter_context(tc.tile_pool(name="work", bufs=3))
        outs = ctx.enter_context(tc.tile_pool(name="outs", bufs=8))
        psum_c = ctx.enter_context(tc.psum_pool(name="psum_c", bufs=1))
        psum_x = ctx.enter_context(tc.psum_pool(name="psum_x", bufs=1))
        psum_m = ctx.enter_context(tc.psum_pool(name="psum_m", bufs=1))
        psum_u = ctx.enter_context(tc.psum_pool(name="psum_u", bufs=2))
        ctx.enter_context(tc.manual_schedule())

        vecs = const.tile([P, 4 * HD], BF16)
        nc.vector.memset(vecs[:], 0.0)
        eps = const.tile([P, 1], F32)
        nc.vector.memset(eps[:], EPS)
        ones = const.tile([P, P], BF16)
        nc.vector.memset(ones[:], 1.0)
        ident = const.tile([P, P], F32)
        make_identity(nc, ident[:])
        warm = const.tile([P, 1], F32)
        nc.scalar.activation(out=warm[:], in_=eps[:], func=ACT.Abs_reciprocal_sqrt)

        def load_w(w, name):
            raw = const.tile([P, PACK, w.shape[1]], BF16, name=name)
            nc.sync.dma_start(out=raw[:], in_=w.rearrange("(p v) c -> p v c", v=PACK))
            return raw

        def load_x(b, pair):
            x_sb = const.tile([P, 2 * D], BF16, name="x_sb%d_%d" % (b, pair))
            nc.sync.dma_start(
                out=x_sb[:], in_=x[b].rearrange("(p h t) k -> h p (t k)", h=2, t=2)[pair]
            )
            return x_sb

        wq_raw = load_w(Wq, "wq_raw")
        x_pairs = [load_x(0, 0)]
        wk_raw = load_w(Wk, "wk_raw")
        wv_raw = load_w(Wv, "wv_raw")
        for n, vec in enumerate((q_gamma, k_gamma, q_beta, k_beta)):
            nc.sync.dma_start(
                out=vecs[0:1, n * HD : (n + 1) * HD], in_=vec.rearrange("(o j) -> o j", o=1)
            )
        cos_sb = const.tile([P, T, HD], BF16)
        nc.sync.dma_start(out=cos_sb[:], in_=cos.rearrange("(p t) j -> p t j", t=T))
        sin_sb = const.tile([P, T, HD], BF16)
        nc.sync.dma_start(out=sin_sb[:], in_=sin.rearrange("(p t) j -> p t j", t=T))
        x_pairs.append(load_x(0, 1))
        x_pairs.extend(load_x(b, pair) for b in range(1, B) for pair in range(2))

        signs = const.tile([P, 3, P], BF16)
        nc.vector.tensor_copy(out=signs[:, 0, :], in_=ident[:])
        nc.vector.tensor_copy(out=signs[:, 1, 0:HALF], in_=ident[:, HALF:HD])
        nc.vector.tensor_copy(out=signs[:, 2, HALF:HD], in_=ident[:, HALF:HD])
        nc.vector.tensor_scalar_mul(out=signs[:, 1, HALF:HD], in0=ident[:, 0:HALF], scalar1=-1.0)
        nc.vector.tensor_scalar_mul(out=signs[:, 2, 0:HALF], in0=ident[:, 0:HALF], scalar1=-1.0)
        ident_b = signs[:, 0, :]
        to_mean = const.tile([P, HEADS], F32)
        nc.vector.tensor_reduce(
            out=to_mean[:],
            in_=ident[:].rearrange("p (h c) -> p h c", c=RUN),
            axis=mybir.AxisListType.X,
            op=ADD,
        )
        nc.vector.tensor_scalar_mul(out=to_mean[:], in0=to_mean[:], scalar1=-1.0 / HD)

        w_grouped = const.tile([P, W_COLS * PACK], BF16, align_bytes=64)
        w_codes = const.tile([P, W_COLS], U32, align_bytes=64)
        w_scales = const.tile([P, W_COLS], U8, align_bytes=64)
        nc.gpsimd.memset(w_scales[:].bitcast(I32), 0)
        m_codes = const.tile([P, W_COLS], U32, align_bytes=64)
        m_scales = const.tile([P, W_COLS], U8, align_bytes=64)

        def regroup_w(copy, raw, first_col, raw_col=0):
            copy(
                out=w_grouped[:, first_col * PACK : (first_col + W_LOAD) * PACK].rearrange(
                    "p (c i v) -> p c v i", i=4, v=PACK
                ),
                in_=raw[:, :, raw_col : raw_col + W_LOAD].rearrange("p v (c i) -> p c v i", i=4),
            )

        def quantise_w(first_col, cols):
            nc.vector.quantize_mx(
                out=w_codes[:, first_col : first_col + cols].bitcast(FP8X4),
                scales=w_scales[:, first_col : first_col + cols],
                in_=w_grouped[:, first_col * PACK : (first_col + cols) * PACK],
            )

        def transpose_x(pair):
            x_words = x_pairs[pair][:].bitcast(F32)
            x_t = psum_x.tile([P, BANK], F32, tag="x", name="x_t")
            for n in range(BANK // P):
                first = (n // 2) * 2 * P + n % 2
                nc.tensor.transpose(
                    x_t[:, n * P : (n + 1) * P],
                    x_words[:, first : first + 2 * P - 1 : 2],
                    ident[:],
                )
            return x_t

        def group_x(copy, x_t):
            grouped = xprep.tile([P, 2 * P * PACK], BF16, align_bytes=64)
            copy(
                out=grouped[:].bitcast(F32).rearrange("p (t r u) -> p t r u", t=2, u=2),
                in_=x_t[:].rearrange("p (t u r) -> p t r u", t=2, u=2),
            )
            return grouped

        x_mx = {}

        def quantise_x(pair, grouped):
            codes = xprep.tile([P, 2 * P], U32, align_bytes=64)
            scales = xprep.tile([P, 2 * P], U8, align_bytes=64)
            nc.vector.quantize_mx(out=codes[:].bitcast(FP8X4), scales=scales[:], in_=grouped[:])
            x_mx[pair] = codes, scales

        sums = {}

        def add_runs(pair, runs):
            if runs[0] == 0:
                sums[pair] = psum_m.tile([P, 2 * P], F32, tag="sums", name="sums")
            codes, scales = x_mx[pair]
            for i in runs:
                cols = slice(i * P, (i + 1) * P)
                nc.tensor.matmul_mx(
                    out=sums[pair][:],
                    lhsT=m_codes[:, cols].bitcast(FP8X4),
                    lhsT_scale=m_scales[:, cols],
                    rhs=codes[:].bitcast(FP8X4),
                    rhs_scale=scales[:],
                    start=i == 0,
                    stop=i == RUNS - 1,
                )

        def keep_sums(pair):
            sums_sb = stats.tile([P, 2 * P], F32)
            nc.scalar.copy(out=sums_sb[:], in_=sums[pair][:])
            return sums_sb

        def make_means(sums_sb, pool, tag):
            means = pool.tile([P, 2, HEADS], F32, tag=tag, name="means")
            for t in range(2):
                nc.tensor.matmul(
                    out=means[:, t, :],
                    lhsT=sums_sb[:, t * P : (t + 1) * P],
                    rhs=to_mean[:],
                    start=True,
                    stop=True,
                )
            neg_mean = stats.tile([P, 2, HEADS], F32)
            nc.scalar.copy(out=neg_mean[:], in_=means[:])
            return neg_mean

        diag = const.tile([P, 4, 2, HD], BF16)
        trig = const.tile([P, 2, T, P], BF16)
        tab_ab = const.tile([P, T, 2, 2, HD], F32)

        def first_ab(spread):
            nc.vector.tensor_tensor(
                out=tab_ab[:, 0, 0],
                in0=spread[:, 0:2, :],
                in1=cos_sb[:, 0:1].to_broadcast([P, 2, HD]),
                op=MULT,
            )
            nc.vector.tensor_tensor(
                out=tab_ab[:, 0, 1, :, 0:HALF],
                in0=spread[:, 0:2, 0:HALF],
                in1=sin_sb[:, 0:1, HALF:HD].to_broadcast([P, 2, HALF]),
                op=MULT,
            )
            nc.vector.scalar_tensor_tensor(
                out=tab_ab[:, 0, 1, :, HALF:HD],
                in0=spread[:, 0:2, HALF:HD],
                scalar=-1.0,
                in1=sin_sb[:, 0:1, 0:HALF].to_broadcast([P, 2, HALF]),
                op0=MULT,
                op1=MULT,
            )

        def make_ab(t):
            nc.gpsimd.tensor_tensor(
                out=tab_ab[:, t, 0],
                in0=gammas[:, 0:2, :],
                in1=cos_sb[:, t : t + 1].to_broadcast([P, 2, HD]),
                op=MULT,
            )
            sin_halves = sin_sb[:, t : t + 1].rearrange("p k (u j) -> p k u j", u=2)
            nc.gpsimd.tensor_tensor(
                out=tab_ab[:, t, 1].rearrange("p k (u j) -> p k u j", u=2),
                in0=signed[:].rearrange("p k (u j) -> p k u j", u=2),
                in1=sin_halves[:, :, ::-1].to_broadcast([P, 2, 2, HALF]),
                op=MULT,
            )

        def diagonals_for_c():
            nc.gpsimd.tensor_tensor(
                out=diag[:, 2],
                in0=signs[:, 0:1, :].to_broadcast([P, 2, HD]),
                in1=gammas[:, 2:4, :],
                op=MULT,
            )
            for to, other in ((slice(0, HALF), slice(HALF, HD)), (slice(HALF, HD), slice(0, HALF))):
                nc.gpsimd.tensor_tensor(
                    out=diag[:, 3, :, to],
                    in0=signs[:, 2:3, to].to_broadcast([P, 2, HALF]),
                    in1=gammas[:, 2:4, other],
                    op=MULT,
                )

        def multiply_c(pair):
            c_bank = psum_c.tile([P, 2, 2, HD], F32, tag="c%d" % pair, name="c_bank")
            for half in range(2):
                for n in range(2):
                    nc.tensor.matmul(
                        out=c_bank[:, half].rearrange("p k j -> p (k j)"),
                        lhsT=trig[:, n, 2 * pair + half, :],
                        rhs=diag[:, 2 + n].rearrange("p k j -> p (k j)"),
                        start=n == 0,
                        stop=n == 1,
                    )
            return c_bank

        gammas = const.tile([P, 4, HD], F32)
        signed = const.tile([P, 2, HD], F32)
        regroup_w(nc.vector.tensor_copy, wq_raw, 0)
        regroup_w(nc.vector.tensor_copy, wq_raw, W_LOAD, W_LOAD)
        regroup_w(nc.scalar.copy, wk_raw, BANK)
        quantise_w(0, BANK)
        x_grouped_0 = group_x(nc.scalar.copy, transpose_x(0))
        spread = psum_c.tile([P, 4, HD], F32, tag="c1")
        nc.tensor.matmul(
            out=spread[:].rearrange("p n j -> p (n j)"), lhsT=ones[:], rhs=vecs[:], start=True, stop=True
        )
        nc.scalar.copy(out=gammas[:], in_=spread[:])
        nc.scalar.copy(out=signed[:, :, 0:HALF], in_=spread[:, 0:2, 0:HALF])
        nc.scalar.activation(
            out=signed[:, :, HALF:HD], in_=spread[:, 0:2, HALF:HD], func=ACT.Copy, scale=-1.0
        )
        regroup_w(nc.vector.tensor_copy, wv_raw, BANK + W_LOAD)
        quantise_w(BANK, BANK)

        def kind_of(h):
            return 0 if h < Q_HEADS else 1

        def project(t, codes, scales):
            token_cols = slice(t % 2 * P, (t % 2 + 1) * P)
            banks = []
            for n, tag in enumerate(("u_q", "u_kv")):
                bank = psum_u.tile([P, BANK], F32, tag=tag, name=tag)
                nc.tensor.matmul_mx(
                    out=bank[:],
                    lhsT=codes[:, token_cols].bitcast(FP8X4),
                    lhsT_scale=scales[:, token_cols],
                    rhs=w_codes[:, n * BANK : (n + 1) * BANK].bitcast(FP8X4),
                    rhs_scale=w_scales[:, n * BANK : (n + 1) * BANK],
                    start=True,
                    stop=True,
                )
                banks.append(bank)
            return banks

        def head_of(banks, h):
            col = (h % Q_HEADS) * HD
            return banks[kind_of(h)][:, col : col + HD]

        def measure(b, t, banks, neg_mean, centred, gp_heads, between=None):
            sum_sq = stats.tile([P, NORMED], F32)
            unread = work.tile([P, NORMED, HD], BF16)
            for h in ORDER:
                if h == 0:
                    for gp_head in gp_heads:
                        nc.scalar.activation(
                            out=centred[:, t % 2, gp_head, :],
                            in_=head_of(banks, gp_head),
                            func=ACT.Identity,
                            bias=neg_mean[:, t % 2, gp_head : gp_head + 1],
                            scale=1.0,
                        )
                nc.scalar.activation(
                    out=unread[:, h, :],
                    in_=head_of(banks, h),
                    func=ACT.Square,
                    bias=neg_mean[:, t % 2, h : h + 1],
                    scale=1.0,
                    accum_out=sum_sq[:, h : h + 1],
                )
                if h == NORMED - 1:
                    v_sb = outs.tile([P, KV_HEADS, HD], F32)
                    nc.scalar.copy(
                        out=v_sb[:].rearrange("p h j -> p (h j)"),
                        in_=banks[1][:, KV_HEADS * HD : BANK],
                    )
                    nc.sync.dma_start(
                        out=out_2[b].rearrange("h (p t) j -> t p h j", t=T)[t], in_=v_sb[:]
                    )
                    if between:
                        between()
            rstd = stats.tile([P, NORMED], F32)
            nc.scalar.activation(
                out=rstd[:],
                in_=sum_sq[:],
                func=ACT.Abs_reciprocal_sqrt,
                bias=eps[:, 0:1],
                scale=1.0 / HD,
            )
            return rstd

        def products(b, t, banks, neg_mean, pair_ab, gp_heads, gp_tables, quantise_now):
            shares = [(h, 2 - gp_tables if h in gp_heads else 2) for h in ORDER]
            mine = [share for share in shares if share[1] > 0]
            for h, tables in mine:
                if b * T + t == 1 and h == 0:
                    x_grouped[2] = group_x(nc.vector.tensor_copy, x_t)
                    quantise_x(2, x_grouped[2])
                if b * T + t == 2 and h == mine[-1][0]:
                    x_grouped[3] = group_x(nc.vector.tensor_copy, x_t)
                if h == mine[1 if b * T + t >= 4 else -1][0]:
                    for pair in quantise_now:
                        quantise_x(pair, x_grouped[pair])
                nc.vector.scalar_tensor_tensor(
                    out=pair_ab[:, t % 2, h, 0:tables, :],
                    in0=head_of(banks, h).unsqueeze(1).to_broadcast([P, tables, HD]),
                    scalar=neg_mean[:, t % 2, h : h + 1],
                    in1=tab_ab[:, t, 0:tables, kind_of(h), :],
                    op0=ADD,
                    op1=MULT,
                )

        def multiply_gp(t0, count, pair_ab, centred, gp_heads, gp_tables):
            mine = slice(t0 % 2, t0 % 2 + count)
            first = 2 - gp_tables
            for h in gp_heads:
                nc.gpsimd.tensor_tensor(
                    out=pair_ab[:, mine, h, first:2],
                    in0=centred[:, mine, h].unsqueeze(2).to_broadcast([P, count, gp_tables, HD]),
                    in1=tab_ab[:, t0 : t0 + count, first:2, 0, :],
                    op=MULT,
                )

        def add_turned(engine, out, ab):
            halves = ab.rearrange("p n k (u j) -> p n k u j", u=2)
            engine.tensor_tensor(
                out=out.rearrange("p n (u j) -> p n u j", u=2),
                in0=halves[:, :, 0],
                in1=halves[:, :, 1, ::-1],
                op=ADD,
            )

        def finish(i, rotated, rstd):
            b, t = divmod(i, T)
            q_sb = outs.tile([P, Q_HEADS, HD], F32)
            k_sb = outs.tile([P, KV_HEADS, HD], F32)
            for h in range(NORMED):
                nc.vector.scalar_tensor_tensor(
                    out=q_sb[:, h, :] if h < Q_HEADS else k_sb[:, h - Q_HEADS, :],
                    in0=rotated[:, t % 2, h, :],
                    scalar=rstd[:, h : h + 1],
                    in1=c_ps[t // 2][:, t % 2, kind_of(h), :],
                    op0=MULT,
                    op1=ADD,
                )
                if h == Q_HEADS - 1:
                    nc.sync.dma_start(
                        out=out_0[b].rearrange("h (p t) j -> t p h j", t=T)[t], in_=q_sb[:]
                    )
            nc.sync.dma_start(out=out_1[b].rearrange("h (p t) j -> t p h j", t=T)[t], in_=k_sb[:])

        quantise_x(0, x_grouped_0)
        banks = {0: project(0, *x_mx[0])}
        x_t = transpose_x(1)
        trig_t = psum_c.tile([P, 2, T, P], BF16, tag="c0")
        for n, table in enumerate((cos_sb, sin_sb)):
            for t in range(T):
                nc.tensor.transpose(trig_t[:, n, t, :], table[:, t, :], ident_b)
        x_grouped = group_x(nc.scalar.copy, x_t)
        for dst, src, per_run in ((m_codes, w_codes, RUN), (m_scales, w_scales, RUN // PACK)):
            nc.vector.tensor_copy(
                out=dst[:].bitcast(I32).rearrange("p (i h c) -> p h i c", h=HEADS, c=per_run),
                in_=src[:].bitcast(I32).rearrange("p (h i c) -> p h i c", h=HEADS, c=per_run),
            )
        add_runs(0, range(RUNS))
        first_sums = const.tile([P, NORMED], F32)
        first_means = const.tile([P, 2, NORMED], F32)
        for part, (heads, bank) in enumerate(((range(0, Q_HEADS), banks[0][0]), (range(Q_HEADS, NORMED), banks[0][1]))):
            nc.vector.tensor_reduce(
                out=first_sums[:, heads.start : heads.stop],
                in_=bank[:, 0 : len(heads) * HD].rearrange("p (h j) -> p h j", j=HD),
                axis=mybir.AxisListType.X,
                op=ADD,
            )
        nc.scalar.activation(out=first_means[:, 0, :], in_=first_sums[:], func=ACT.Copy, scale=-1.0 / HD)
        first_ab(spread)
        nc.vector.tensor_copy(out=trig[:], in_=trig_t[:])
        quantise_x(1, x_grouped)
        x_grouped = {}
        diagonals_for_c()
        for t in range(1, T):
            make_ab(t)
        neg_means = {}
        banks[1] = project(1, *x_mx[0])
        c_ps = []
        waiting = []
        for i in range(TILES):
            b, t = divmod(i, T)
            pair, side = divmod(i, 2)
            if side == 0:
                pair_ab = work.tile([P, 2, NORMED, 2, HD], F32)
                centred = work.tile([P, 2, Q_HEADS, HD], F32)
                rotated = work.tile([P, 2, NORMED, HD], F32)
            if i not in banks:
                banks[i] = project(t, *x_mx[pair])
            gp_heads = GP_HEADS if i in SHARED else ()
            neg_mean = neg_means[pair] if i > 0 else first_means
            kept = []
            rstd = measure(b, t, banks[i], neg_mean, centred, gp_heads, (lambda: kept.append(keep_sums(i))) if i < 2 else None)
            if i < 2:
                neg_means[i] = make_means(kept[0], psum_c, "c0")
            if i == 0:
                add_runs(1, range(RUNS))
                x_t = transpose_x(2)

            if i == 4:
                x_grouped[4] = group_x(nc.scalar.copy, transpose_x(4))
            if side == 0 and 0 < pair < PAIRS - 1:
                if pair >= 2:
                    add_runs(pair + 1, range(RUNS // 2 if pair > 2 else 0, RUNS))
                sums_sb = keep_sums(pair + 1)
            if side == 1 and 0 < pair < PAIRS - 1:
                pool, tag = (psum_c, "c1") if i < 4 else (psum_m, "sums")
                neg_means[pair + 1] = make_means(sums_sb, pool, tag)
            if side == 1 and 2 <= pair < PAIRS - 3:
                x_grouped[pair + 3] = group_x(nc.scalar.copy, transpose_x(pair + 3))
            if i == 1:
                banks[2] = project(2, *x_mx[1])
            if i == 2:
                banks[3] = project(3, *x_mx[1])
                x_t = transpose_x(3)
            if i == 3:
                banks[4] = project(4, *x_mx[2])
            if i in (2, 3):
                c_ps.append(multiply_c(i - 2))

            quantise_now = ()
            if side == 1 and 1 <= pair < PAIRS - 2:
                quantise_now = (pair + 2,)
            gp_tables = 2
            products(b, t, banks[i], neg_mean, pair_ab, gp_heads, gp_tables, quantise_now)
            waiting.append((i, rotated, rstd))
            if i == 1:
                add_runs(2, range(RUNS))
            if side == 1 and 2 <= pair < PAIRS - 2:
                banks[i + 1] = project((t + 1) % T, *x_mx[pair + 1])
                add_runs(pair + 2, range(RUNS // 2))
            single = TILES - 2 <= i
            if single or side == 1:
                mine = slice(side, side + 1) if single else slice(0, 2)
                if gp_heads:
                    multiply_gp(
                        t if single else t - 1, mine.stop - mine.start, pair_ab, centred, gp_heads, gp_tables
                    )
                for heads in (slice(0, 4), slice(4, 6)) if i == TILES - 1 else (slice(0, NORMED),):
                    add_turned(
                        nc.gpsimd,
                        rotated[:, mine, heads].rearrange("p t h j -> p (t h) j"),
                        pair_ab[:, mine, heads].rearrange("p t h n j -> p (t h) n j"),
                    )
            while len(waiting) > LAG:
                finish(*waiting[0])
                waiting = waiting[1:]
        for tile in waiting:
            finish(*tile)
